import numpy as np
import ml_dtypes


def mxq(x, axis, fmt="e4m3"):
    dtype, down = {"e4m3": (ml_dtypes.float8_e4m3fn, 7), "e5m2": (ml_dtypes.float8_e5m2, 14)}[fmt]
    v = np.moveaxis(np.asarray(x, np.float32).astype(ml_dtypes.bfloat16).astype(np.float64), axis, -1)
    blocks = v.reshape(v.shape[:-1] + (-1, 32))
    amax = np.abs(blocks).max(-1, keepdims=True)
    byte = np.maximum(np.where(amax > 0, np.frexp(amax)[1] - 1 + 127, 0) - down, 1)
    scale = np.exp2(byte - 127.0)
    codes = (blocks / scale).astype(np.float32).astype(dtype).astype(np.float64)
    return np.moveaxis((codes * scale).reshape(v.shape), -1, axis)


WIDE = False


def mx_kscale(k):
    if not WIDE:
        return np.ones(k)
    levels = np.array([20, -20, 10, -10, 0])
    a = np.random.permutation(np.resize(levels, k // 512 * 4)).reshape(k // 512, 4)
    idx = np.arange(k)
    return np.exp2(a[idx // 512, idx % 128 // 32])


BF16 = ml_dtypes.bfloat16


def bf(x):
    return np.asarray(x, np.float32).astype(BF16)


def f64(x):
    return np.asarray(x).astype(np.float64)


M, NI, NO, G, P = 8192, 128, 512, 5, 3
NB = G + P


def sigmoid(v):
    return 1.0 / (1.0 + np.exp(-v))


def silu(v):
    return v * sigmoid(v)


def b_spline(x, t, p):
    xc = np.clip(x, t[P], t[-P - 1])[..., None]
    n_int = t.shape[0] - 1
    b = np.where((xc >= t[:-1]) & (xc < t[1:]), 1.0, 0.0)
    for j in range(1, p + 1):
        nv = n_int - j
        ti = t[:nv]
        ti_j = t[j:nv + j]
        ti1 = t[1:nv + 1]
        ti_j1 = t[j + 1:nv + j + 1]
        a1 = (xc - ti) / np.maximum(ti_j - ti, 1e-8)
        a2 = (ti_j1 - xc) / np.maximum(ti_j1 - ti1, 1e-8)
        b = a1 * b[..., :nv] + a2 * b[..., 1:nv + 1]
    return b


def setup_inputs():
    h = 2.0 / G
    grid = np.linspace(-1.0, 1.0, G + 1)
    knots = bf(np.concatenate([grid[0] - h * np.arange(P, 0, -1), grid, grid[-1] + h * np.arange(1, P + 1)]))
    kb = f64(knots)
    u = mx_kscale(NO)
    x = f64(bf(np.random.standard_normal((M, NI))))
    x = bf(np.where((x == kb[P]) | (x == kb[-P - 1]), x * 0.9375, x))
    c0 = bf(np.random.standard_normal((NI, NO, NB)) * 2.0 / np.sqrt(NI))
    w0 = bf(np.random.uniform(-1.0, 1.0, (NI, NO)) * 1.5 / np.sqrt(NI))
    g = bf(np.random.standard_normal((M, NO)) * np.exp2(np.random.randint(-12, 1, (M, 1))) * 4.0 * u)
    z = f64(x) @ f64(w0)
    return {"x": x, "coeff": bf(f64(c0) / u[None, :, None]), "base_weight": bf(f64(w0) / u[None, :]),
            "knots": knots, "z": np.asarray(z, np.float32), "grad_out": g}


def reference(x, coeff, base_weight, knots, z, grad_out):
    x = f64(x)
    t = f64(knots)
    zf = f64(z)
    g = f64(grad_out)
    sg = sigmoid(zf)
    dz = g * (sg * (1.0 + zf * (1.0 - sg)))
    a = mxq(dz, 1, "e5m2") @ mxq(f64(base_weight), 1, "e4m3").T
    cq = mxq(f64(coeff).transpose(1, 0, 2).reshape(NO, NI * NB), 0, "e4m3")
    s = (mxq(g, 1, "e5m2") @ cq).reshape(M, NI, NB)
    b2 = b_spline(x, t, P - 1)
    db = P * (b2[..., :NB] / (t[P:P + NB] - t[:NB]) - b2[..., 1:NB + 1] / (t[P + 1:P + NB + 1] - t[1:NB + 1]))
    m = np.where((x > t[P]) & (x < t[-P - 1]), 1.0, 0.0)
    return a + m * (db * s).sum(axis=2)

@@ -1,0 +1,351 @@
+from contextlib import ExitStack
+
+import concourse.mybir as mybir
+from concourse.masks import make_identity
+
+F32 = mybir.dt.float32
+BF16 = mybir.dt.bfloat16
+U32 = mybir.dt.uint32
+U8 = mybir.dt.uint8
+E4M3_X4 = mybir.dt.float8_e4m3fn_x4
+E5M2_X4 = mybir.dt.float8_e5m2_x4
+ALU = mybir.AluOpType
+ACT = mybir.ActivationFunctionType
+
+P = 128
+TOKENS = 8192
+N_OUT = 512
+N_BASIS = 8
+N_KNOTS = 12
+LO = 3
+HI = 8
+PACK = 4
+GROUP = 512
+TILES = GROUP // P
+N_GROUPS = TOKENS // GROUP
+HALF = GROUP // 2
+HUGE = 3.0e38
+
+FLOPS = 2 * TOKENS * N_OUT * (P * N_BASIS + P)
+
+
+def spline_tables(nc, consts, knots):
+    knots_bf = consts.tile([P, N_KNOTS], BF16)
+    nc.sync.dma_start(out=knots_bf[:], in_=knots.partition_broadcast(P))
+    t = consts.tile([P, N_KNOTS], F32)
+    nc.vector.tensor_copy(out=t[:], in_=knots_bf[:])
+    neg_t = consts.tile([P, N_KNOTS], F32)
+    nc.vector.tensor_scalar(out=neg_t[:], in0=t[:], scalar1=-1.0, scalar2=None, op0=ALU.mult)
+
+    from_lo = consts.tile([P, N_KNOTS], F32)
+    from_hi = consts.tile([P, N_KNOTS], F32)
+    neg_from_lo = consts.tile([P, N_KNOTS], F32)
+    neg_from_hi = consts.tile([P, N_KNOTS], F32)
+    for end, plain, negative in ((LO, from_lo, neg_from_lo), (HI, from_hi, neg_from_hi)):
+        nc.vector.tensor_scalar(
+            out=plain[:], in0=t[:], scalar1=t[:, end : end + 1], scalar2=None, op0=ALU.subtract
+        )
+        nc.vector.tensor_scalar(
+            out=negative[:], in0=plain[:], scalar1=-1.0, scalar2=None, op0=ALU.mult
+        )
+
+    gap = []
+    for d in range(1, 5):
+        gap_d = consts.tile([P, N_KNOTS - d], F32, name="gap%d" % d)
+        nc.vector.tensor_tensor(
+            out=gap_d[:], in0=t[:, d:N_KNOTS], in1=t[:, 0 : N_KNOTS - d], op=ALU.subtract
+        )
+        gap.append(gap_d)
+
+    size = consts.tile([P, 5, N_BASIS], F32)
+    for j in range(5):
+        factors = [gap[j - l - 1][:, l : l + N_BASIS] for l in range(j)]
+        factors += [gap[l - j - 1][:, j : j + N_BASIS] for l in range(j + 1, 5)]
+        nc.vector.tensor_tensor(out=size[:, j, :], in0=factors[0], in1=factors[1], op=ALU.mult)
+        for factor in factors[2:]:
+            nc.vector.tensor_tensor(out=size[:, j, :], in0=size[:, j, :], in1=factor, op=ALU.mult)
+    inverse = consts.tile([P, 5, N_BASIS], F32)
+    nc.vector.reciprocal(out=inverse[:], in_=size[:])
+
+    span = gap[3]
+    lead = consts.tile([P, N_BASIS], F32)
+    nc.vector.scalar_tensor_tensor(
+        out=lead[:, 0:4], in0=inverse[:, 4, 0:4], scalar=-3.0, in1=span[:, 0:4],
+        op0=ALU.mult, op1=ALU.mult,
+    )
+    nc.vector.scalar_tensor_tensor(
+        out=lead[:, 4:8], in0=inverse[:, 0, 4:8], scalar=3.0, in1=span[:, 4:8],
+        op0=ALU.mult, op1=ALU.mult,
+    )
+    ratio = consts.tile([P, 5, N_BASIS], F32)
+    for j in range(1, 4):
+        sign = -1.0 if j % 2 else 1.0
+        nc.vector.scalar_tensor_tensor(
+            out=ratio[:, j, 0:4], in0=inverse[:, j, 0:4], scalar=sign, in1=size[:, 4, 0:4],
+            op0=ALU.mult, op1=ALU.mult,
+        )
+        nc.vector.scalar_tensor_tensor(
+            out=ratio[:, j, 4:8], in0=inverse[:, j, 4:8], scalar=sign, in1=size[:, 0, 4:8],
+            op0=ALU.mult, op1=ALU.mult,
+        )
+    return {
+        "neg_t": neg_t, "from_lo": from_lo, "from_hi": from_hi,
+        "neg_from_lo": neg_from_lo, "neg_from_hi": neg_from_hi, "lead": lead, "ratio": ratio,
+    }
+
+
+def tile_bsplinekanlayer_t_v_kernel(tc, x, coeff, base_weight, knots, z, grad_out, out):
+    nc = tc.nc
+    with ExitStack() as stack:
+        consts = stack.enter_context(tc.tile_pool(name="consts", bufs=1))
+        loads = stack.enter_context(tc.tile_pool(name="loads", bufs=3))
+        gates = stack.enter_context(tc.tile_pool(name="gates", bufs=3))
+        grouped = stack.enter_context(tc.tile_pool(name="grouped", bufs=2))
+        quantised = stack.enter_context(tc.tile_pool(name="quantised", bufs=2))
+        shapes = stack.enter_context(tc.tile_pool(name="shapes", bufs=2))
+        terms = stack.enter_context(tc.tile_pool(name="terms", bufs=2))
+        results = stack.enter_context(tc.tile_pool(name="results", bufs=2))
+        psum_in = stack.enter_context(tc.psum_pool(name="psum_in", bufs=3))
+        psum_mx = stack.enter_context(tc.psum_pool(name="psum_mx", bufs=3))
+        psum_out = stack.enter_context(tc.psum_pool(name="psum_out", bufs=2))
+
+        ident_bf = consts.tile([P, P], BF16)
+        make_identity(nc, ident_bf[:])
+        ident_f32 = consts.tile([P, P], F32)
+        make_identity(nc, ident_f32[:])
+
+        tables = spline_tables(nc, consts, knots)
+
+        coeff_sb = consts.tile([P, N_OUT, N_BASIS], BF16)
+        nc.sync.dma_start(out=coeff_sb[:], in_=coeff)
+        weight_sb = consts.tile([P, N_OUT], BF16)
+        nc.sync.dma_start(out=weight_sb[:], in_=base_weight)
+        coeff_by_r = consts.tile([P, N_BASIS * N_OUT], BF16)
+        sorted_view = coeff_by_r[:].rearrange("p (r o) -> p r o", r=N_BASIS)
+        nc.vector.tensor_copy(
+            out=sorted_view[:, 0:4, :], in_=coeff_sb[:, :, 0:4].rearrange("p o r -> p r o")
+        )
+        nc.scalar.copy(
+            out=sorted_view[:, 4:8, :], in_=coeff_sb[:, :, 4:8].rearrange("p o r -> p r o")
+        )
+        coeff_words = coeff_by_r[:].bitcast(F32)
+
+        coeff_grouped = consts.tile([P, N_BASIS * P * PACK], BF16, align_bytes=64)
+        coeff_grouped_words = coeff_grouped[:].bitcast(F32).rearrange("p (n u) -> p n u", u=2)
+        coeff_codes = consts.tile([P, N_BASIS * P], U32, align_bytes=64)
+        coeff_scales = consts.tile([P, N_BASIS * P], U8, align_bytes=64)
+        for pair in range(N_BASIS // 2):
+            coeff_t = psum_in.tile([P, 2, 2, P], F32, tag="in")
+            for rr in range(2):
+                for u in range(2):
+                    first = (2 * pair + rr) * (N_OUT // 2) + u * P
+                    nc.tensor.transpose(
+                        out=coeff_t[:, rr, u, :], in_=coeff_words[:, first : first + P],
+                        identity=ident_f32[:],
+                    )
+            cols = slice(pair * 2 * P, (pair + 1) * 2 * P)
+            nc.vector.tensor_copy(
+                out=coeff_grouped_words[:, cols, :].rearrange("p (r i) u -> p r i u", r=2),
+                in_=coeff_t[:].rearrange("p r u i -> p r i u"),
+            )
+            nc.vector.quantize_mx(
+                out=coeff_codes[:, cols].bitcast(E4M3_X4),
+                scales=coeff_scales[:, cols],
+                in_=coeff_grouped[:, pair * 2 * P * PACK : (pair + 1) * 2 * P * PACK],
+            )
+
+        weight_t = psum_in.tile([P, PACK, P], BF16, tag="in")
+        for c in range(PACK):
+            nc.tensor.transpose(
+                out=weight_t[:, c, :], in_=weight_sb[:, c * P : (c + 1) * P], identity=ident_bf[:]
+            )
+        weight_grouped = consts.tile([P, P * PACK], BF16, align_bytes=64)
+        nc.vector.tensor_copy(
+            out=weight_grouped[:].rearrange("p (i c) -> p i c", c=PACK),
+            in_=weight_t[:].rearrange("p c i -> p i c"),
+        )
+        weight_codes = consts.tile([P, P], U32, align_bytes=64)
+        weight_scales = consts.tile([P, P], U8, align_bytes=64)
+        nc.vector.quantize_mx(
+            out=weight_codes[:].bitcast(E4M3_X4), scales=weight_scales[:], in_=weight_grouped[:]
+        )
+
+        for j in range(N_GROUPS):
+            rows = slice(j * GROUP, (j + 1) * GROUP)
+            x_sb = loads.tile([P, TILES, P], BF16)
+            nc.sync.dma_start(out=x_sb[:], in_=x[rows, :].rearrange("(p t) i -> p t i", t=TILES))
+            g_sb = loads.tile([P, TILES * N_OUT], BF16)
+            nc.sync.dma_start(
+                out=g_sb[:], in_=grad_out[rows, :].rearrange("(p t) o -> p (t o)", t=TILES)
+            )
+            z_sb = loads.tile([P, TILES * N_OUT], F32)
+            nc.sync.dma_start(out=z_sb[:], in_=z[rows, :].rearrange("(p t) o -> p (t o)", t=TILES))
+
+            x_t = psum_in.tile([P, TILES, P], BF16, tag="in")
+            for t in range(TILES):
+                nc.tensor.transpose(out=x_t[:, t, :], in_=x_sb[:, t, :], identity=ident_bf[:])
+            x_flat = x_t[:].rearrange("p t k -> p (t k)")
+            above_lo = shapes.tile([P, GROUP], F32)
+            below_hi = shapes.tile([P, GROUP], F32)
+            nc.scalar.activation(
+                out=above_lo[:], in_=x_flat, func=ACT.Identity, bias=tables["neg_t"][:, LO : LO + 1]
+            )
+            nc.scalar.activation(
+                out=below_hi[:], in_=x_flat, func=ACT.Identity, bias=tables["neg_t"][:, HI : HI + 1]
+            )
+            nc.vector.scalar_tensor_tensor(
+                out=above_lo[:], in0=above_lo[:], scalar=tables["from_lo"][:, HI : HI + 1],
+                in1=above_lo[:], op0=ALU.is_lt, op1=ALU.mult,
+            )
+            nc.vector.scalar_tensor_tensor(
+                out=below_hi[:], in0=below_hi[:], scalar=tables["from_hi"][:, LO : LO + 1],
+                in1=below_hi[:], op0=ALU.is_gt, op1=ALU.mult,
+            )
+
+            rise = {}
+            fall = {}
+            for k in range(LO + 1, HI):
+                rise[k] = shapes.tile([P, GROUP], F32, name="rise%d" % k)
+                nc.gpsimd.tensor_scalar(
+                    out=rise[k][:], in0=above_lo[:], scalar1=HUGE,
+                    scalar2=tables["from_lo"][:, k : k + 1], op0=ALU.min, op1=ALU.max,
+                )
+                nc.scalar.activation(
+                    out=rise[k][:], in_=rise[k][:], func=ACT.Square,
+                    bias=tables["neg_from_lo"][:, k : k + 1],
+                )
+                fall[k] = shapes.tile([P, GROUP], F32, name="fall%d" % k)
+                nc.gpsimd.tensor_scalar(
+                    out=fall[k][:], in0=below_hi[:], scalar1=tables["from_hi"][:, k : k + 1],
+                    scalar2=-HUGE, op0=ALU.min, op1=ALU.max,
+                )
+                nc.scalar.activation(
+                    out=fall[k][:], in_=fall[k][:], func=ACT.Square,
+                    bias=tables["neg_from_hi"][:, k : k + 1],
+                )
+
+            for r in range(4, 7):
+                for k in range(r + 1, HI):
+                    nc.vector.scalar_tensor_tensor(
+                        out=rise[r][:], in0=rise[k][:], scalar=tables["ratio"][:, k - r, r : r + 1],
+                        in1=rise[r][:], op0=ALU.mult, op1=ALU.add,
+                    )
+                    mr = 7 - r
+                    mk = 11 - k
+                    nc.vector.scalar_tensor_tensor(
+                        out=fall[mr + 4][:], in0=fall[mk][:],
+                        scalar=tables["ratio"][:, mk - mr, mr : mr + 1],
+                        in1=fall[mr + 4][:], op0=ALU.mult, op1=ALU.add,
+                    )
+
+            g_words = g_sb[:].bitcast(F32)
+            g_grouped = grouped.tile([P, GROUP * PACK], BF16, align_bytes=64)
+            g_grouped_words = g_grouped[:].bitcast(F32).rearrange("p (n u) -> p n u", u=2)
+            for half in range(2):
+                g_t = psum_in.tile([P, 2, 2, P], F32, tag="in")
+                for tt in range(2):
+                    for u in range(2):
+                        first = (2 * half + tt) * (N_OUT // 2) + u * P
+                        nc.tensor.transpose(
+                            out=g_t[:, tt, u, :], in_=g_words[:, first : first + P],
+                            identity=ident_f32[:],
+                        )
+                nc.scalar.copy(
+                    out=g_grouped_words[:, half * HALF : (half + 1) * HALF, :].rearrange(
+                        "p (t k) u -> p t k u", t=2
+                    ),
+                    in_=g_t[:].rearrange("p t u k -> p t k u"),
+                )
+            g_codes = quantised.tile([P, GROUP], U32, align_bytes=64)
+            g_scales = quantised.tile([P, GROUP], U8, align_bytes=64)
+            nc.vector.quantize_mx(
+                out=g_codes[:].bitcast(E5M2_X4), scales=g_scales[:], in_=g_grouped[:]
+            )
+
+            dz_grouped = grouped.tile([P, GROUP * PACK], BF16, align_bytes=64)
+            dz_grouped_view = dz_grouped[:].rearrange("p (n c) -> p n c", c=PACK)
+            for half in range(2):
+                cols = slice(half * 2 * N_OUT, (half + 1) * 2 * N_OUT)
+                tanh_part = gates.tile([P, 2 * N_OUT], F32)
+                silu_part = gates.tile([P, 2 * N_OUT], F32)
+                nc.scalar.activation(out=tanh_part[:], in_=z_sb[:, cols], func=ACT.Tanh, scale=-0.5)
+                nc.scalar.activation(out=silu_part[:], in_=z_sb[:, cols], func=ACT.Silu, scale=-1.0)
+                nc.vector.scalar_tensor_tensor(
+                    out=tanh_part[:], in0=tanh_part[:], scalar=1.0, in1=g_sb[:, cols],
+                    op0=ALU.subtract, op1=ALU.mult,
+                )
+                twice_dz = gates.tile([P, 2 * N_OUT], BF16)
+                nc.vector.scalar_tensor_tensor(
+                    out=twice_dz[:], in0=silu_part[:], scalar=1.0, in1=tanh_part[:],
+                    op0=ALU.subtract, op1=ALU.mult,
+                )
+                dz_t = psum_in.tile([P, 2, PACK, P], BF16, tag="in")
+                for tt in range(2):
+                    for c in range(PACK):
+                        first = tt * N_OUT + c * P
+                        nc.tensor.transpose(
+                            out=dz_t[:, tt, c, :], in_=twice_dz[:, first : first + P],
+                            identity=ident_bf[:],
+                        )
+                nc.scalar.activation(
+                    out=dz_grouped_view[:, half * HALF : (half + 1) * HALF, :].rearrange(
+                        "p (t k) c -> p t k c", t=2
+                    ),
+                    in_=dz_t[:].rearrange("p t c k -> p t k c"),
+                    func=ACT.Copy, scale=0.5,
+                )
+            dz_codes = quantised.tile([P, GROUP], U32, align_bytes=64)
+            dz_scales = quantised.tile([P, GROUP], U8, align_bytes=64)
+            nc.vector.quantize_mx(
+                out=dz_codes[:].bitcast(E5M2_X4), scales=dz_scales[:], in_=dz_grouped[:]
+            )
+
+            summands = []
+            for r in range(N_BASIS):
+                s_bank = psum_mx.tile([P, GROUP], F32, tag="mx")
+                nc.tensor.matmul_mx(
+                    out=s_bank[:],
+                    lhsT=coeff_codes[:, r * P : (r + 1) * P].bitcast(E4M3_X4),
+                    lhsT_scale=coeff_scales[:, r * P : (r + 1) * P],
+                    rhs=g_codes[:].bitcast(E5M2_X4),
+                    rhs_scale=g_scales[:],
+                    start=True,
+                    stop=True,
+                )
+                shape = rise[r] if r >= 4 else fall[r + 4]
+                term = terms.tile([P, GROUP], F32, name="term%d" % r)
+                nc.vector.scalar_tensor_tensor(
+                    out=term[:], in0=s_bank[:], scalar=tables["lead"][:, r : r + 1], in1=shape[:],
+                    op0=ALU.mult, op1=ALU.mult,
+                )
+                summands.append(term)
+            a_bank = psum_mx.tile([P, GROUP], F32, tag="mx")
+            nc.tensor.matmul_mx(
+                out=a_bank[:],
+                lhsT=weight_codes[:].bitcast(E4M3_X4),
+                lhsT_scale=weight_scales[:],
+                rhs=dz_codes[:].bitcast(E5M2_X4),
+                rhs_scale=dz_scales[:],
+                start=True,
+                stop=True,
+            )
+            a_term = terms.tile([P, GROUP], F32)
+            nc.scalar.copy(out=a_term[:], in_=a_bank[:])
+            summands.append(a_term)
+
+            total = psum_out.tile([P, TILES, P], F32)
+            for t in range(TILES):
+                for n, summand in enumerate(summands):
+                    nc.tensor.matmul(
+                        out=total[:, t, :],
+                        lhsT=summand[:, t * P : (t + 1) * P],
+                        rhs=ident_f32[:],
+                        is_transpose=True,
+                        start=(n == 0),
+                        stop=(n == len(summands) - 1),
+                    )
+            out_sb = results.tile([P, TILES, P], F32)
+            nc.scalar.copy(out=out_sb[:], in_=total[:])
+            nc.sync.dma_start(
+                out=out[rows, :].rearrange("(p t) i -> p t i", t=TILES), in_=out_sb[:]
+            )

@@ -26,29 +26,16 @@ N_GROUPS = TOKENS // GROUP
 HALF = GROUP // 2
 HUGE = 3.0e38
 
+DROPPED = 3
+KEPT = (0, 1, 2, 4, 5, 6, 7)
+NEGATED = 8
+BASE = 9
+N_PARTS = 10
+
 FLOPS = 2 * TOKENS * N_OUT * (P * N_BASIS + P)
 
 
-def spline_tables(nc, consts, knots):
-    knots_bf = consts.tile([P, N_KNOTS], BF16)
-    nc.sync.dma_start(out=knots_bf[:], in_=knots.partition_broadcast(P))
-    t = consts.tile([P, N_KNOTS], F32)
-    nc.vector.tensor_copy(out=t[:], in_=knots_bf[:])
-    neg_t = consts.tile([P, N_KNOTS], F32)
-    nc.vector.tensor_scalar(out=neg_t[:], in0=t[:], scalar1=-1.0, scalar2=None, op0=ALU.mult)
-
-    from_lo = consts.tile([P, N_KNOTS], F32)
-    from_hi = consts.tile([P, N_KNOTS], F32)
-    neg_from_lo = consts.tile([P, N_KNOTS], F32)
-    neg_from_hi = consts.tile([P, N_KNOTS], F32)
-    for end, plain, negative in ((LO, from_lo, neg_from_lo), (HI, from_hi, neg_from_hi)):
-        nc.vector.tensor_scalar(
-            out=plain[:], in0=t[:], scalar1=t[:, end : end + 1], scalar2=None, op0=ALU.subtract
-        )
-        nc.vector.tensor_scalar(
-            out=negative[:], in0=plain[:], scalar1=-1.0, scalar2=None, op0=ALU.mult
-        )
-
+def spline_weights(nc, consts, t):
     gap = []
     for d in range(1, 5):
         gap_d = consts.tile([P, N_KNOTS - d], F32, name="gap%d" % d)
@@ -69,29 +56,19 @@ def spline_tables(nc, consts, knots):
 
     span = gap[3]
     lead = consts.tile([P, N_BASIS], F32)
-    nc.vector.scalar_tensor_tensor(
-        out=lead[:, 0:4], in0=inverse[:, 4, 0:4], scalar=-3.0, in1=span[:, 0:4],
-        op0=ALU.mult, op1=ALU.mult,
-    )
-    nc.vector.scalar_tensor_tensor(
-        out=lead[:, 4:8], in0=inverse[:, 0, 4:8], scalar=3.0, in1=span[:, 4:8],
-        op0=ALU.mult, op1=ALU.mult,
-    )
     ratio = consts.tile([P, 5, N_BASIS], F32)
-    for j in range(1, 4):
-        sign = -1.0 if j % 2 else 1.0
+    for splines, leading, degree in ((slice(0, 4), 4, -3.0), (slice(4, 8), 0, 3.0)):
         nc.vector.scalar_tensor_tensor(
-            out=ratio[:, j, 0:4], in0=inverse[:, j, 0:4], scalar=sign, in1=size[:, 4, 0:4],
-            op0=ALU.mult, op1=ALU.mult,
+            out=lead[:, splines], in0=inverse[:, leading, splines], scalar=degree,
+            in1=span[:, splines], op0=ALU.mult, op1=ALU.mult,
         )
-        nc.vector.scalar_tensor_tensor(
-            out=ratio[:, j, 4:8], in0=inverse[:, j, 4:8], scalar=sign, in1=size[:, 0, 4:8],
-            op0=ALU.mult, op1=ALU.mult,
-        )
-    return {
-        "neg_t": neg_t, "from_lo": from_lo, "from_hi": from_hi,
-        "neg_from_lo": neg_from_lo, "neg_from_hi": neg_from_hi, "lead": lead, "ratio": ratio,
-    }
+        for j in range(1, 4):
+            nc.vector.scalar_tensor_tensor(
+                out=ratio[:, j, splines], in0=inverse[:, j, splines],
+                scalar=(-1.0 if j % 2 else 1.0), in1=size[:, leading, splines],
+                op0=ALU.mult, op1=ALU.mult,
+            )
+    return lead, ratio
 
 
 def tile_bsplinekanlayer_t_v_kernel(tc, x, coeff, base_weight, knots, z, grad_out, out):
@@ -99,145 +76,66 @@ def tile_bsplinekanlayer_t_v_kernel(tc, x, coeff, base_weight, knots, z, grad_ou
     with ExitStack() as stack:
         consts = stack.enter_context(tc.tile_pool(name="consts", bufs=1))
         loads = stack.enter_context(tc.tile_pool(name="loads", bufs=3))
-        gates = stack.enter_context(tc.tile_pool(name="gates", bufs=3))
+        masked = stack.enter_context(tc.tile_pool(name="masked", bufs=2))
+        gates = stack.enter_context(tc.tile_pool(name="gates", bufs=2))
         grouped = stack.enter_context(tc.tile_pool(name="grouped", bufs=2))
         quantised = stack.enter_context(tc.tile_pool(name="quantised", bufs=2))
-        shapes = stack.enter_context(tc.tile_pool(name="shapes", bufs=2))
+        squares = stack.enter_context(tc.tile_pool(name="squares", bufs=2))
         terms = stack.enter_context(tc.tile_pool(name="terms", bufs=2))
         results = stack.enter_context(tc.tile_pool(name="results", bufs=2))
-        psum_in = stack.enter_context(tc.psum_pool(name="psum_in", bufs=3))
-        psum_mx = stack.enter_context(tc.psum_pool(name="psum_mx", bufs=3))
-        psum_out = stack.enter_context(tc.psum_pool(name="psum_out", bufs=2))
+        psum_x = stack.enter_context(tc.psum_pool(name="psum_x", bufs=1))
+        psum_in = stack.enter_context(tc.psum_pool(name="psum_in", bufs=2))
+        psum_mx = stack.enter_context(tc.psum_pool(name="psum_mx", bufs=4))
+        psum_out = stack.enter_context(tc.psum_pool(name="psum_out", bufs=1))
+        stack.enter_context(tc.manual_schedule())
 
-        ident_bf = consts.tile([P, P], BF16)
-        make_identity(nc, ident_bf[:])
-        ident_f32 = consts.tile([P, P], F32)
-        make_identity(nc, ident_f32[:])
+        loaded = {}
+        x_transposed = {}
+        gate_parts = {}
+        operands = {}
+        shapes = {}
+        summands = {}
 
-        tables = spline_tables(nc, consts, knots)
-
-        coeff_sb = consts.tile([P, N_OUT, N_BASIS], BF16)
-        nc.sync.dma_start(out=coeff_sb[:], in_=coeff)
-        weight_sb = consts.tile([P, N_OUT], BF16)
-        nc.sync.dma_start(out=weight_sb[:], in_=base_weight)
-        coeff_by_r = consts.tile([P, N_BASIS * N_OUT], BF16)
-        sorted_view = coeff_by_r[:].rearrange("p (r o) -> p r o", r=N_BASIS)
-        nc.vector.tensor_copy(
-            out=sorted_view[:, 0:4, :], in_=coeff_sb[:, :, 0:4].rearrange("p o r -> p r o")
-        )
-        nc.scalar.copy(
-            out=sorted_view[:, 4:8, :], in_=coeff_sb[:, :, 4:8].rearrange("p o r -> p r o")
-        )
-        coeff_words = coeff_by_r[:].bitcast(F32)
-
-        coeff_grouped = consts.tile([P, N_BASIS * P * PACK], BF16, align_bytes=64)
-        coeff_grouped_words = coeff_grouped[:].bitcast(F32).rearrange("p (n u) -> p n u", u=2)
-        coeff_codes = consts.tile([P, N_BASIS * P], U32, align_bytes=64)
-        coeff_scales = consts.tile([P, N_BASIS * P], U8, align_bytes=64)
-        for pair in range(N_BASIS // 2):
-            coeff_t = psum_in.tile([P, 2, 2, P], F32, tag="in")
-            for rr in range(2):
-                for u in range(2):
-                    first = (2 * pair + rr) * (N_OUT // 2) + u * P
-                    nc.tensor.transpose(
-                        out=coeff_t[:, rr, u, :], in_=coeff_words[:, first : first + P],
-                        identity=ident_f32[:],
-                    )
-            cols = slice(pair * 2 * P, (pair + 1) * 2 * P)
-            nc.vector.tensor_copy(
-                out=coeff_grouped_words[:, cols, :].rearrange("p (r i) u -> p r i u", r=2),
-                in_=coeff_t[:].rearrange("p r u i -> p r i u"),
-            )
-            nc.vector.quantize_mx(
-                out=coeff_codes[:, cols].bitcast(E4M3_X4),
-                scales=coeff_scales[:, cols],
-                in_=coeff_grouped[:, pair * 2 * P * PACK : (pair + 1) * 2 * P * PACK],
-            )
-
-        weight_t = psum_in.tile([P, PACK, P], BF16, tag="in")
-        for c in range(PACK):
-            nc.tensor.transpose(
-                out=weight_t[:, c, :], in_=weight_sb[:, c * P : (c + 1) * P], identity=ident_bf[:]
-            )
-        weight_grouped = consts.tile([P, P * PACK], BF16, align_bytes=64)
-        nc.vector.tensor_copy(
-            out=weight_grouped[:].rearrange("p (i c) -> p i c", c=PACK),
-            in_=weight_t[:].rearrange("p c i -> p i c"),
-        )
-        weight_codes = consts.tile([P, P], U32, align_bytes=64)
-        weight_scales = consts.tile([P, P], U8, align_bytes=64)
-        nc.vector.quantize_mx(
-            out=weight_codes[:].bitcast(E4M3_X4), scales=weight_scales[:], in_=weight_grouped[:]
-        )
-
-        for j in range(N_GROUPS):
+        def load(j):
             rows = slice(j * GROUP, (j + 1) * GROUP)
-            x_sb = loads.tile([P, TILES, P], BF16)
-            nc.sync.dma_start(out=x_sb[:], in_=x[rows, :].rearrange("(p t) i -> p t i", t=TILES))
+            x_sb = loads.tile([P, GROUP], BF16)
+            nc.sync.dma_start(out=x_sb[:], in_=x[rows, :].rearrange("(p t) i -> p (t i)", t=TILES))
             g_sb = loads.tile([P, TILES * N_OUT], BF16)
             nc.sync.dma_start(
                 out=g_sb[:], in_=grad_out[rows, :].rearrange("(p t) o -> p (t o)", t=TILES)
             )
             z_sb = loads.tile([P, TILES * N_OUT], F32)
             nc.sync.dma_start(out=z_sb[:], in_=z[rows, :].rearrange("(p t) o -> p (t o)", t=TILES))
+            loaded[j] = (x_sb, g_sb, z_sb)
 
-            x_t = psum_in.tile([P, TILES, P], BF16, tag="in")
-            for t in range(TILES):
-                nc.tensor.transpose(out=x_t[:, t, :], in_=x_sb[:, t, :], identity=ident_bf[:])
-            x_flat = x_t[:].rearrange("p t k -> p (t k)")
-            above_lo = shapes.tile([P, GROUP], F32)
-            below_hi = shapes.tile([P, GROUP], F32)
-            nc.scalar.activation(
-                out=above_lo[:], in_=x_flat, func=ACT.Identity, bias=tables["neg_t"][:, LO : LO + 1]
+        def mask_and_transpose_x(j):
+            x_sb = loaded[j][0]
+            push = masked.tile([P, 2, GROUP], BF16)
+            x_masked = masked.tile([P, 2, GROUP], BF16)
+            nc.vector.tensor_scalar(
+                out=push[:, 0, :], in0=x_sb[:], scalar1=t[:, HI : HI + 1], scalar2=-HUGE,
+                op0=ALU.is_ge, op1=ALU.mult,
             )
-            nc.scalar.activation(
-                out=below_hi[:], in_=x_flat, func=ACT.Identity, bias=tables["neg_t"][:, HI : HI + 1]
+            nc.vector.tensor_scalar(
+                out=push[:, 1, :], in0=x_sb[:], scalar1=t[:, LO : LO + 1], scalar2=HUGE,
+                op0=ALU.is_le, op1=ALU.mult,
             )
-            nc.vector.scalar_tensor_tensor(
-                out=above_lo[:], in0=above_lo[:], scalar=tables["from_lo"][:, HI : HI + 1],
-                in1=above_lo[:], op0=ALU.is_lt, op1=ALU.mult,
-            )
-            nc.vector.scalar_tensor_tensor(
-                out=below_hi[:], in0=below_hi[:], scalar=tables["from_hi"][:, LO : LO + 1],
-                in1=below_hi[:], op0=ALU.is_gt, op1=ALU.mult,
-            )
-
-            rise = {}
-            fall = {}
-            for k in range(LO + 1, HI):
-                rise[k] = shapes.tile([P, GROUP], F32, name="rise%d" % k)
-                nc.gpsimd.tensor_scalar(
-                    out=rise[k][:], in0=above_lo[:], scalar1=HUGE,
-                    scalar2=tables["from_lo"][:, k : k + 1], op0=ALU.min, op1=ALU.max,
+            x_t = psum_x.tile([P, 2, GROUP], BF16)
+            for copy in range(2):
+                nc.vector.tensor_tensor(
+                    out=x_masked[:, copy, :], in0=x_sb[:], in1=push[:, copy, :], op=ALU.add
                 )
-                nc.scalar.activation(
-                    out=rise[k][:], in_=rise[k][:], func=ACT.Square,
-                    bias=tables["neg_from_lo"][:, k : k + 1],
-                )
-                fall[k] = shapes.tile([P, GROUP], F32, name="fall%d" % k)
-                nc.gpsimd.tensor_scalar(
-                    out=fall[k][:], in0=below_hi[:], scalar1=tables["from_hi"][:, k : k + 1],
-                    scalar2=-HUGE, op0=ALU.min, op1=ALU.max,
-                )
-                nc.scalar.activation(
-                    out=fall[k][:], in_=fall[k][:], func=ACT.Square,
-                    bias=tables["neg_from_hi"][:, k : k + 1],
-                )
-
-            for r in range(4, 7):
-                for k in range(r + 1, HI):
-                    nc.vector.scalar_tensor_tensor(
-                        out=rise[r][:], in0=rise[k][:], scalar=tables["ratio"][:, k - r, r : r + 1],
-                        in1=rise[r][:], op0=ALU.mult, op1=ALU.add,
+            for copy in range(2):
+                for tt in range(TILES):
+                    cols = slice(tt * P, (tt + 1) * P)
+                    nc.tensor.transpose(
+                        out=x_t[:, copy, cols], in_=x_masked[:, copy, cols], identity=ident_bf[:]
                     )
-                    mr = 7 - r
-                    mk = 11 - k
-                    nc.vector.scalar_tensor_tensor(
-                        out=fall[mr + 4][:], in0=fall[mk][:],
-                        scalar=tables["ratio"][:, mk - mr, mr : mr + 1],
-                        in1=fall[mr + 4][:], op0=ALU.mult, op1=ALU.add,
-                    )
+            x_transposed[j] = x_t
 
+        def transpose_g_and_z(j):
+            g_sb = loaded[j][1]
+            z_sb = loaded[j][2]
             g_words = g_sb[:].bitcast(F32)
             g_grouped = grouped.tile([P, GROUP * PACK], BF16, align_bytes=64)
             g_grouped_words = g_grouped[:].bitcast(F32).rearrange("p (n u) -> p n u", u=2)
@@ -256,96 +154,215 @@ def tile_bsplinekanlayer_t_v_kernel(tc, x, coeff, base_weight, knots, z, grad_ou
                     ),
                     in_=g_t[:].rearrange("p t u k -> p t k u"),
                 )
+            z_view = z_sb[:].rearrange("p (t u q e) -> p t u e q", t=TILES, u=2, e=2)
+            tanh_part = gates.tile([P, GROUP * PACK], F32)
+            silu_part = gates.tile([P, GROUP * PACK], F32)
+            for tt in range(TILES):
+                z_t = psum_in.tile([P, PACK, P], F32, tag="in")
+                for u in range(2):
+                    for e in range(2):
+                        nc.tensor.transpose(
+                            out=z_t[:, 2 * u + e, :], in_=z_view[:, tt, u, e, :],
+                            identity=ident_f32[:],
+                        )
+                cols = slice(tt * P * PACK, (tt + 1) * P * PACK)
+                nc.scalar.activation(
+                    out=tanh_part[:, cols].rearrange("p (k c) -> p k c", c=PACK),
+                    in_=z_t[:].rearrange("p c k -> p k c"), func=ACT.Tanh, scale=-0.5,
+                )
+                nc.scalar.activation(
+                    out=silu_part[:, cols].rearrange("p (k c) -> p k c", c=PACK),
+                    in_=z_t[:].rearrange("p c k -> p k c"), func=ACT.Silu, scale=-1.0,
+                )
+            gate_parts[j] = (g_grouped, tanh_part, silu_part)
+
+        def gate_and_quantise(j):
+            g_grouped, tanh_part, silu_part = gate_parts[j]
+            twice_dz = grouped.tile([P, GROUP * PACK], BF16, align_bytes=64)
+            halves = (slice(0, HALF * PACK), slice(HALF * PACK, GROUP * PACK))
+            for cols in halves:
+                nc.vector.scalar_tensor_tensor(
+                    out=tanh_part[:, cols], in0=tanh_part[:, cols], scalar=1.0,
+                    in1=g_grouped[:, cols], op0=ALU.subtract, op1=ALU.mult,
+                )
+            for cols in halves:
+                nc.vector.scalar_tensor_tensor(
+                    out=twice_dz[:, cols], in0=silu_part[:, cols], scalar=1.0,
+                    in1=tanh_part[:, cols], op0=ALU.subtract, op1=ALU.mult,
+                )
             g_codes = quantised.tile([P, GROUP], U32, align_bytes=64)
             g_scales = quantised.tile([P, GROUP], U8, align_bytes=64)
             nc.vector.quantize_mx(
                 out=g_codes[:].bitcast(E5M2_X4), scales=g_scales[:], in_=g_grouped[:]
             )
-
-            dz_grouped = grouped.tile([P, GROUP * PACK], BF16, align_bytes=64)
-            dz_grouped_view = dz_grouped[:].rearrange("p (n c) -> p n c", c=PACK)
-            for half in range(2):
-                cols = slice(half * 2 * N_OUT, (half + 1) * 2 * N_OUT)
-                tanh_part = gates.tile([P, 2 * N_OUT], F32)
-                silu_part = gates.tile([P, 2 * N_OUT], F32)
-                nc.scalar.activation(out=tanh_part[:], in_=z_sb[:, cols], func=ACT.Tanh, scale=-0.5)
-                nc.scalar.activation(out=silu_part[:], in_=z_sb[:, cols], func=ACT.Silu, scale=-1.0)
-                nc.vector.scalar_tensor_tensor(
-                    out=tanh_part[:], in0=tanh_part[:], scalar=1.0, in1=g_sb[:, cols],
-                    op0=ALU.subtract, op1=ALU.mult,
-                )
-                twice_dz = gates.tile([P, 2 * N_OUT], BF16)
-                nc.vector.scalar_tensor_tensor(
-                    out=twice_dz[:], in0=silu_part[:], scalar=1.0, in1=tanh_part[:],
-                    op0=ALU.subtract, op1=ALU.mult,
-                )
-                dz_t = psum_in.tile([P, 2, PACK, P], BF16, tag="in")
-                for tt in range(2):
-                    for c in range(PACK):
-                        first = tt * N_OUT + c * P
-                        nc.tensor.transpose(
-                            out=dz_t[:, tt, c, :], in_=twice_dz[:, first : first + P],
-                            identity=ident_bf[:],
-                        )
-                nc.scalar.activation(
-                    out=dz_grouped_view[:, half * HALF : (half + 1) * HALF, :].rearrange(
-                        "p (t k) c -> p t k c", t=2
-                    ),
-                    in_=dz_t[:].rearrange("p t c k -> p t k c"),
-                    func=ACT.Copy, scale=0.5,
-                )
             dz_codes = quantised.tile([P, GROUP], U32, align_bytes=64)
             dz_scales = quantised.tile([P, GROUP], U8, align_bytes=64)
             nc.vector.quantize_mx(
-                out=dz_codes[:].bitcast(E5M2_X4), scales=dz_scales[:], in_=dz_grouped[:]
+                out=dz_codes[:].bitcast(E5M2_X4), scales=dz_scales[:], in_=twice_dz[:]
             )
+            operands[j] = (g_codes, g_scales, dz_codes, dz_scales)
 
-            summands = []
-            for r in range(N_BASIS):
-                s_bank = psum_mx.tile([P, GROUP], F32, tag="mx")
-                nc.tensor.matmul_mx(
-                    out=s_bank[:],
-                    lhsT=coeff_codes[:, r * P : (r + 1) * P].bitcast(E4M3_X4),
-                    lhsT_scale=coeff_scales[:, r * P : (r + 1) * P],
-                    rhs=g_codes[:].bitcast(E5M2_X4),
-                    rhs_scale=g_scales[:],
-                    start=True,
-                    stop=True,
+        def truncated_squares(j):
+            x_t = x_transposed[j]
+            rise = {}
+            fall = {}
+            for k in range(LO + 1, HI):
+                rise[k] = squares.tile([P, GROUP], F32, name="rise%d" % k)
+                nc.scalar.activation(
+                    out=rise[k][:], in_=x_t[:, 0, :], func=ACT.Relu, bias=neg_t[:, k : k + 1]
                 )
+            for k in range(LO + 1, HI - 1):
+                fall[k] = squares.tile([P, GROUP], F32, name="fall%d" % k)
+                nc.scalar.activation(
+                    out=fall[k][:], in_=x_t[:, 1, :], func=ACT.Relu, scale=-1.0,
+                    bias=t[:, k : k + 1],
+                )
+            for k in range(LO + 1, HI):
+                nc.scalar.activation(out=rise[k][:], in_=rise[k][:], func=ACT.Square)
+            for k in range(LO + 1, HI - 1):
+                nc.scalar.activation(out=fall[k][:], in_=fall[k][:], func=ACT.Square)
+            shapes[j] = (rise, fall)
+
+        def combine_squares(j):
+            rise, fall = shapes[j]
+            rise_steps = [(rise[r], rise[k], k - r, r) for r in range(4, 7) for k in range(r + 1, HI)]
+            fall_steps = [
+                (fall[r + 4], fall[k], k - r, r) for r in (2, 1) for k in range(LO + 1, r + 4)
+            ]
+            steps = []
+            for n, step in enumerate(rise_steps):
+                steps.append(step)
+                steps.extend(fall_steps[n : n + 1])
+            for target, square, jj, r in steps:
+                nc.vector.scalar_tensor_tensor(
+                    out=target[:], in0=square[:], scalar=ratio[:, jj, r : r + 1], in1=target[:],
+                    op0=ALU.mult, op1=ALU.add,
+                )
+
+        def part(n):
+            cols = slice(n * P, (n + 1) * P)
+            return weight_codes[:, cols].bitcast(E4M3_X4), weight_scales[:, cols]
+
+        def multiply(j):
+            g_codes, g_scales, dz_codes, dz_scales = operands[j]
+            rise, fall = shapes[j]
+            a_bank = psum_mx.tile([P, GROUP], F32, tag="mx")
+            codes, scales = part(BASE)
+            nc.tensor.matmul_mx(
+                out=a_bank[:], lhsT=codes, lhsT_scale=scales,
+                rhs=dz_codes[:].bitcast(E5M2_X4), rhs_scale=dz_scales[:], start=True, stop=True,
+            )
+            a_term = terms.tile([P, GROUP], F32)
+            nc.scalar.activation(out=a_term[:], in_=a_bank[:], func=ACT.Copy, scale=0.5)
+            summands[j] = [a_term]
+            for r in KEPT:
+                s_bank = psum_mx.tile([P, GROUP], F32, tag="mx")
+                for n in (r, NEGATED):
+                    codes, scales = part(n)
+                    nc.tensor.matmul_mx(
+                        out=s_bank[:], lhsT=codes, lhsT_scale=scales,
+                        rhs=g_codes[:].bitcast(E5M2_X4), rhs_scale=g_scales[:],
+                        start=(n == r), stop=(n == NEGATED),
+                    )
                 shape = rise[r] if r >= 4 else fall[r + 4]
                 term = terms.tile([P, GROUP], F32, name="term%d" % r)
                 nc.vector.scalar_tensor_tensor(
-                    out=term[:], in0=s_bank[:], scalar=tables["lead"][:, r : r + 1], in1=shape[:],
+                    out=term[:], in0=s_bank[:], scalar=lead[:, r : r + 1], in1=shape[:],
                     op0=ALU.mult, op1=ALU.mult,
                 )
-                summands.append(term)
-            a_bank = psum_mx.tile([P, GROUP], F32, tag="mx")
-            nc.tensor.matmul_mx(
-                out=a_bank[:],
-                lhsT=weight_codes[:].bitcast(E4M3_X4),
-                lhsT_scale=weight_scales[:],
-                rhs=dz_codes[:].bitcast(E5M2_X4),
-                rhs_scale=dz_scales[:],
-                start=True,
-                stop=True,
-            )
-            a_term = terms.tile([P, GROUP], F32)
-            nc.scalar.copy(out=a_term[:], in_=a_bank[:])
-            summands.append(a_term)
+                summands[j].append(term)
 
+        def add_up_and_store(j):
             total = psum_out.tile([P, TILES, P], F32)
-            for t in range(TILES):
-                for n, summand in enumerate(summands):
+            last = len(summands[j]) - 1
+            for tt in range(TILES):
+                for n, summand in enumerate(summands[j]):
                     nc.tensor.matmul(
-                        out=total[:, t, :],
-                        lhsT=summand[:, t * P : (t + 1) * P],
-                        rhs=ident_f32[:],
-                        is_transpose=True,
-                        start=(n == 0),
-                        stop=(n == len(summands) - 1),
+                        out=total[:, tt, :], lhsT=summand[:, tt * P : (tt + 1) * P],
+                        rhs=ident_f32[:], is_transpose=True, start=(n == 0), stop=(n == last),
                     )
             out_sb = results.tile([P, TILES, P], F32)
             nc.scalar.copy(out=out_sb[:], in_=total[:])
+            rows = slice(j * GROUP, (j + 1) * GROUP)
             nc.sync.dma_start(
                 out=out[rows, :].rearrange("(p t) i -> p t i", t=TILES), in_=out_sb[:]
             )
+
+        knots_bf = consts.tile([P, N_KNOTS], BF16)
+        nc.sync.dma_start(out=knots_bf[:], in_=knots.partition_broadcast(P))
+        load(0)
+        coeff_sb = consts.tile([P, N_OUT, N_BASIS], BF16)
+        nc.sync.dma_start(out=coeff_sb[:], in_=coeff)
+        weight_sb = consts.tile([P, N_PARTS * N_OUT], BF16)
+        weight_view = weight_sb[:].rearrange("p (n o) -> p n o", n=N_PARTS)
+        nc.sync.dma_start(out=weight_view[:, BASE, :], in_=base_weight)
+        load(1)
+
+        ident_bf = consts.tile([P, P], BF16)
+        make_identity(nc, ident_bf[:])
+        ident_f32 = consts.tile([P, P], F32)
+        make_identity(nc, ident_f32[:])
+
+        transpose_g_and_z(0)
+
+        t = consts.tile([P, N_KNOTS], F32)
+        nc.vector.tensor_copy(out=t[:], in_=knots_bf[:])
+        neg_t = consts.tile([P, N_KNOTS], F32)
+        nc.vector.tensor_scalar(out=neg_t[:], in0=t[:], scalar1=-1.0, scalar2=None, op0=ALU.mult)
+        mask_and_transpose_x(0)
+        lead, ratio = spline_weights(nc, consts, t)
+
+        nc.vector.tensor_copy(
+            out=weight_view[:, 0:4, :], in_=coeff_sb[:, :, 0:4].rearrange("p o r -> p r o")
+        )
+        nc.scalar.copy(
+            out=weight_view[:, 4:8, :], in_=coeff_sb[:, :, 4:8].rearrange("p o r -> p r o")
+        )
+        nc.vector.tensor_scalar(
+            out=weight_view[:, NEGATED, :], in0=coeff_sb[:, :, DROPPED], scalar1=-1.0, scalar2=None,
+            op0=ALU.mult,
+        )
+        weight_words = weight_sb[:].bitcast(F32)
+        weight_grouped = consts.tile([P, N_PARTS * P * PACK], BF16, align_bytes=64)
+        weight_grouped_words = weight_grouped[:].bitcast(F32).rearrange("p (n u) -> p n u", u=2)
+        weight_codes = consts.tile([P, N_PARTS * P], U32, align_bytes=64)
+        weight_scales = consts.tile([P, N_PARTS * P], U8, align_bytes=64)
+        for pair in range(N_PARTS // 2):
+            weight_t = psum_in.tile([P, 2, 2, P], F32, tag="in")
+            for nn in range(2):
+                for u in range(2):
+                    first = (2 * pair + nn) * (N_OUT // 2) + u * P
+                    nc.tensor.transpose(
+                        out=weight_t[:, nn, u, :], in_=weight_words[:, first : first + P],
+                        identity=ident_f32[:],
+                    )
+            nc.vector.tensor_copy(
+                out=weight_grouped_words[:, pair * 2 * P : (pair + 1) * 2 * P, :].rearrange(
+                    "p (n i) u -> p n i u", n=2
+                ),
+                in_=weight_t[:].rearrange("p n u i -> p n i u"),
+            )
+        for pair in range(N_PARTS // 2):
+            cols = slice(pair * 2 * P, (pair + 1) * 2 * P)
+            nc.vector.quantize_mx(
+                out=weight_codes[:, cols].bitcast(E4M3_X4),
+                scales=weight_scales[:, cols],
+                in_=weight_grouped[:, pair * 2 * P * PACK : (pair + 1) * 2 * P * PACK],
+            )
+
+        for i in range(N_GROUPS + 1):
+            if i >= 1:
+                multiply(i - 1)
+            if i + 2 < N_GROUPS:
+                load(i + 2)
+            if i < N_GROUPS:
+                truncated_squares(i)
+            if i >= 1:
+                add_up_and_store(i - 1)
+            if i < N_GROUPS:
+                gate_and_quantise(i)
+            if i + 1 < N_GROUPS:
+                mask_and_transpose_x(i + 1)
+                transpose_g_and_z(i + 1)
+            if i < N_GROUPS:
+                combine_squares(i)

@@ -95,6 +95,9 @@ def tile_bsplinekanlayer_t_v_kernel(tc, x, coeff, base_weight, knots, z, grad_ou
         operands = {}
         shapes = {}
         summands = {}
+        x_pushed = {}
+        doubled = {}
+        totals = {}
 
         def load(j):
             rows = slice(j * GROUP, (j + 1) * GROUP)
@@ -108,7 +111,10 @@ def tile_bsplinekanlayer_t_v_kernel(tc, x, coeff, base_weight, knots, z, grad_ou
             nc.sync.dma_start(out=z_sb[:], in_=z[rows, :].rearrange("(p t) o -> p (t o)", t=TILES))
             loaded[j] = (x_sb, g_sb, z_sb)
 
-        def mask_and_transpose_x(j):
+        def share(count, piece, pieces):
+            return range(count * piece // pieces, count * (piece + 1) // pieces)
+
+        def mask_x(j):
             x_sb = loaded[j][0]
             push = masked.tile([P, 2, GROUP], BF16)
             x_masked = masked.tile([P, 2, GROUP], BF16)
@@ -120,23 +126,24 @@ def tile_bsplinekanlayer_t_v_kernel(tc, x, coeff, base_weight, knots, z, grad_ou
                 out=push[:, 1, :], in0=x_sb[:], scalar1=t[:, LO : LO + 1], scalar2=HUGE,
                 op0=ALU.is_le, op1=ALU.mult,
             )
-            x_t = psum_x.tile([P, 2, GROUP], BF16)
             for copy in range(2):
                 nc.vector.tensor_tensor(
                     out=x_masked[:, copy, :], in0=x_sb[:], in1=push[:, copy, :], op=ALU.add
                 )
+            x_pushed[j] = x_masked
+
+        def transpose_x(j):
+            x_t = psum_x.tile([P, 2, GROUP], BF16)
             for copy in range(2):
                 for tt in range(TILES):
                     cols = slice(tt * P, (tt + 1) * P)
                     nc.tensor.transpose(
-                        out=x_t[:, copy, cols], in_=x_masked[:, copy, cols], identity=ident_bf[:]
+                        out=x_t[:, copy, cols], in_=x_pushed[j][:, copy, cols], identity=ident_bf[:]
                     )
             x_transposed[j] = x_t
 
-        def transpose_g_and_z(j):
-            g_sb = loaded[j][1]
-            z_sb = loaded[j][2]
-            g_words = g_sb[:].bitcast(F32)
+        def transpose_g(j):
+            g_words = loaded[j][1][:].bitcast(F32)
             g_grouped = grouped.tile([P, GROUP * PACK], BF16, align_bytes=64)
             g_grouped_words = g_grouped[:].bitcast(F32).rearrange("p (n u) -> p n u", u=2)
             for half in range(2):
@@ -154,10 +161,15 @@ def tile_bsplinekanlayer_t_v_kernel(tc, x, coeff, base_weight, knots, z, grad_ou
                     ),
                     in_=g_t[:].rearrange("p t u k -> p t k u"),
                 )
-            z_view = z_sb[:].rearrange("p (t u q e) -> p t u e q", t=TILES, u=2, e=2)
             tanh_part = gates.tile([P, GROUP * PACK], F32)
             silu_part = gates.tile([P, GROUP * PACK], F32)
-            for tt in range(TILES):
+            gate_parts[j] = (g_grouped, tanh_part, silu_part)
+
+        def transpose_z(j, half):
+            z_view = loaded[j][2][:].rearrange("p (t u q e) -> p t u e q", t=TILES, u=2, e=2)
+            tanh_part = gate_parts[j][1]
+            silu_part = gate_parts[j][2]
+            for tt in (2 * half, 2 * half + 1):
                 z_t = psum_in.tile([P, PACK, P], F32, tag="in")
                 for u in range(2):
                     for e in range(2):
@@ -174,56 +186,61 @@ def tile_bsplinekanlayer_t_v_kernel(tc, x, coeff, base_weight, knots, z, grad_ou
                     out=silu_part[:, cols].rearrange("p (k c) -> p k c", c=PACK),
                     in_=z_t[:].rearrange("p c k -> p k c"), func=ACT.Silu, scale=-1.0,
                 )
-            gate_parts[j] = (g_grouped, tanh_part, silu_part)
 
-        def gate_and_quantise(j):
+        def gate(j, factor):
             g_grouped, tanh_part, silu_part = gate_parts[j]
-            twice_dz = grouped.tile([P, GROUP * PACK], BF16, align_bytes=64)
-            halves = (slice(0, HALF * PACK), slice(HALF * PACK, GROUP * PACK))
-            for cols in halves:
-                nc.vector.scalar_tensor_tensor(
-                    out=tanh_part[:, cols], in0=tanh_part[:, cols], scalar=1.0,
-                    in1=g_grouped[:, cols], op0=ALU.subtract, op1=ALU.mult,
-                )
-            for cols in halves:
-                nc.vector.scalar_tensor_tensor(
-                    out=twice_dz[:, cols], in0=silu_part[:, cols], scalar=1.0,
-                    in1=tanh_part[:, cols], op0=ALU.subtract, op1=ALU.mult,
-                )
+            if factor == 1:
+                twice_dz = grouped.tile([P, GROUP * PACK], BF16, align_bytes=64)
+                doubled[j] = twice_dz
+            for cols in (slice(0, HALF * PACK), slice(HALF * PACK, GROUP * PACK)):
+                if factor == 0:
+                    nc.vector.scalar_tensor_tensor(
+                        out=tanh_part[:, cols], in0=tanh_part[:, cols], scalar=1.0,
+                        in1=g_grouped[:, cols], op0=ALU.subtract, op1=ALU.mult,
+                    )
+                else:
+                    nc.vector.scalar_tensor_tensor(
+                        out=doubled[j][:, cols], in0=silu_part[:, cols], scalar=1.0,
+                        in1=tanh_part[:, cols], op0=ALU.subtract, op1=ALU.mult,
+                    )
+
+        def quantise(j):
             g_codes = quantised.tile([P, GROUP], U32, align_bytes=64)
             g_scales = quantised.tile([P, GROUP], U8, align_bytes=64)
             nc.vector.quantize_mx(
-                out=g_codes[:].bitcast(E5M2_X4), scales=g_scales[:], in_=g_grouped[:]
+                out=g_codes[:].bitcast(E5M2_X4), scales=g_scales[:], in_=gate_parts[j][0][:]
             )
             dz_codes = quantised.tile([P, GROUP], U32, align_bytes=64)
             dz_scales = quantised.tile([P, GROUP], U8, align_bytes=64)
             nc.vector.quantize_mx(
-                out=dz_codes[:].bitcast(E5M2_X4), scales=dz_scales[:], in_=twice_dz[:]
+                out=dz_codes[:].bitcast(E5M2_X4), scales=dz_scales[:], in_=doubled[j][:]
             )
             operands[j] = (g_codes, g_scales, dz_codes, dz_scales)
 
-        def truncated_squares(j):
+        def truncated_squares(j, quarter):
+            if quarter == 0:
+                rise = {}
+                fall = {}
+                for k in range(LO + 1, HI):
+                    rise[k] = squares.tile([P, GROUP], F32, name="rise%d" % k)
+                for k in range(LO + 1, HI - 1):
+                    fall[k] = squares.tile([P, GROUP], F32, name="fall%d" % k)
+                shapes[j] = (rise, fall)
+            rise, fall = shapes[j]
             x_t = x_transposed[j]
-            rise = {}
-            fall = {}
-            for k in range(LO + 1, HI):
-                rise[k] = squares.tile([P, GROUP], F32, name="rise%d" % k)
-                nc.scalar.activation(
-                    out=rise[k][:], in_=x_t[:, 0, :], func=ACT.Relu, bias=neg_t[:, k : k + 1]
-                )
-            for k in range(LO + 1, HI - 1):
-                fall[k] = squares.tile([P, GROUP], F32, name="fall%d" % k)
-                nc.scalar.activation(
-                    out=fall[k][:], in_=x_t[:, 1, :], func=ACT.Relu, scale=-1.0,
-                    bias=t[:, k : k + 1],
-                )
-            for k in range(LO + 1, HI):
-                nc.scalar.activation(out=rise[k][:], in_=rise[k][:], func=ACT.Square)
-            for k in range(LO + 1, HI - 1):
-                nc.scalar.activation(out=fall[k][:], in_=fall[k][:], func=ACT.Square)
-            shapes[j] = (rise, fall)
+            ramps = [(rise[k], x_t[:, 0, :], 1.0, neg_t[:, k : k + 1]) for k in range(LO + 1, HI)]
+            ramps += [(fall[k], x_t[:, 1, :], -1.0, t[:, k : k + 1]) for k in range(LO + 1, HI - 1)]
+            for n in share(2 * len(ramps), quarter, 4):
+                if n < len(ramps):
+                    square, source, sign, shift = ramps[n]
+                    nc.scalar.activation(
+                        out=square[:], in_=source, func=ACT.Relu, scale=sign, bias=shift
+                    )
+                else:
+                    square = ramps[n - len(ramps)][0]
+                    nc.scalar.activation(out=square[:], in_=square[:], func=ACT.Square)
 
-        def combine_squares(j):
+        def combine_squares(j, quarter):
             rise, fall = shapes[j]
             rise_steps = [(rise[r], rise[k], k - r, r) for r in range(4, 7) for k in range(r + 1, HI)]
             fall_steps = [
@@ -233,7 +250,8 @@ def tile_bsplinekanlayer_t_v_kernel(tc, x, coeff, base_weight, knots, z, grad_ou
             for n, step in enumerate(rise_steps):
                 steps.append(step)
                 steps.extend(fall_steps[n : n + 1])
-            for target, square, jj, r in steps:
+            for n in share(len(steps), quarter, 4):
+                target, square, jj, r = steps[n]
                 nc.vector.scalar_tensor_tensor(
                     out=target[:], in0=square[:], scalar=ratio[:, jj, r : r + 1], in1=target[:],
                     op0=ALU.mult, op1=ALU.add,
@@ -243,50 +261,52 @@ def tile_bsplinekanlayer_t_v_kernel(tc, x, coeff, base_weight, knots, z, grad_ou
             cols = slice(n * P, (n + 1) * P)
             return weight_codes[:, cols].bitcast(E4M3_X4), weight_scales[:, cols]
 
-        def multiply(j):
+        def multiply(j, n_term):
             g_codes, g_scales, dz_codes, dz_scales = operands[j]
             rise, fall = shapes[j]
-            a_bank = psum_mx.tile([P, GROUP], F32, tag="mx")
-            codes, scales = part(BASE)
-            nc.tensor.matmul_mx(
-                out=a_bank[:], lhsT=codes, lhsT_scale=scales,
-                rhs=dz_codes[:].bitcast(E5M2_X4), rhs_scale=dz_scales[:], start=True, stop=True,
-            )
-            a_term = terms.tile([P, GROUP], F32)
-            nc.scalar.activation(out=a_term[:], in_=a_bank[:], func=ACT.Copy, scale=0.5)
-            summands[j] = [a_term]
-            for r in KEPT:
-                s_bank = psum_mx.tile([P, GROUP], F32, tag="mx")
+            bank = psum_mx.tile([P, GROUP], F32, tag="mx")
+            term = terms.tile([P, GROUP], F32, name="term%d" % n_term)
+            if n_term == 0:
+                codes, scales = part(BASE)
+                nc.tensor.matmul_mx(
+                    out=bank[:], lhsT=codes, lhsT_scale=scales,
+                    rhs=dz_codes[:].bitcast(E5M2_X4), rhs_scale=dz_scales[:], start=True, stop=True,
+                )
+                nc.scalar.activation(out=term[:], in_=bank[:], func=ACT.Copy, scale=0.5)
+                summands[j] = [term]
+            else:
+                r = KEPT[n_term - 1]
                 for n in (r, NEGATED):
                     codes, scales = part(n)
                     nc.tensor.matmul_mx(
-                        out=s_bank[:], lhsT=codes, lhsT_scale=scales,
+                        out=bank[:], lhsT=codes, lhsT_scale=scales,
                         rhs=g_codes[:].bitcast(E5M2_X4), rhs_scale=g_scales[:],
                         start=(n == r), stop=(n == NEGATED),
                     )
                 shape = rise[r] if r >= 4 else fall[r + 4]
-                term = terms.tile([P, GROUP], F32, name="term%d" % r)
                 nc.vector.scalar_tensor_tensor(
-                    out=term[:], in0=s_bank[:], scalar=lead[:, r : r + 1], in1=shape[:],
+                    out=term[:], in0=bank[:], scalar=lead[:, r : r + 1], in1=shape[:],
                     op0=ALU.mult, op1=ALU.mult,
                 )
                 summands[j].append(term)
 
-        def add_up_and_store(j):
-            total = psum_out.tile([P, TILES, P], F32)
+        def add_up(j, tt):
+            if tt == 0:
+                total = psum_out.tile([P, TILES, P], F32)
+                totals[j] = total
             last = len(summands[j]) - 1
-            for tt in range(TILES):
-                for n, summand in enumerate(summands[j]):
-                    nc.tensor.matmul(
-                        out=total[:, tt, :], lhsT=summand[:, tt * P : (tt + 1) * P],
-                        rhs=ident_f32[:], is_transpose=True, start=(n == 0), stop=(n == last),
-                    )
-            out_sb = results.tile([P, TILES, P], F32)
-            nc.scalar.copy(out=out_sb[:], in_=total[:])
-            rows = slice(j * GROUP, (j + 1) * GROUP)
-            nc.sync.dma_start(
-                out=out[rows, :].rearrange("(p t) i -> p t i", t=TILES), in_=out_sb[:]
-            )
+            for n, summand in enumerate(summands[j]):
+                nc.tensor.matmul(
+                    out=totals[j][:, tt, :], lhsT=summand[:, tt * P : (tt + 1) * P],
+                    rhs=ident_f32[:], is_transpose=True, start=(n == 0), stop=(n == last),
+                )
+            if tt == TILES - 1:
+                out_sb = results.tile([P, TILES, P], F32)
+                nc.scalar.copy(out=out_sb[:], in_=totals[j][:])
+                rows = slice(j * GROUP, (j + 1) * GROUP)
+                nc.sync.dma_start(
+                    out=out[rows, :].rearrange("(p t) i -> p t i", t=TILES), in_=out_sb[:]
+                )
 
         knots_bf = consts.tile([P, N_KNOTS], BF16)
         nc.sync.dma_start(out=knots_bf[:], in_=knots.partition_broadcast(P))
@@ -303,13 +323,16 @@ def tile_bsplinekanlayer_t_v_kernel(tc, x, coeff, base_weight, knots, z, grad_ou
         ident_f32 = consts.tile([P, P], F32)
         make_identity(nc, ident_f32[:])
 
-        transpose_g_and_z(0)
+        transpose_g(0)
+        transpose_z(0, 0)
+        transpose_z(0, 1)
 
         t = consts.tile([P, N_KNOTS], F32)
         nc.vector.tensor_copy(out=t[:], in_=knots_bf[:])
         neg_t = consts.tile([P, N_KNOTS], F32)
         nc.vector.tensor_scalar(out=neg_t[:], in0=t[:], scalar1=-1.0, scalar2=None, op0=ALU.mult)
-        mask_and_transpose_x(0)
+        mask_x(0)
+        transpose_x(0)
         lead, ratio = spline_weights(nc, consts, t)
 
         nc.vector.tensor_copy(
@@ -350,19 +373,29 @@ def tile_bsplinekanlayer_t_v_kernel(tc, x, coeff, base_weight, knots, z, grad_ou
                 in_=weight_grouped[:, pair * 2 * P * PACK : (pair + 1) * 2 * P * PACK],
             )
 
-        for i in range(N_GROUPS + 1):
-            if i >= 1:
-                multiply(i - 1)
-            if i + 2 < N_GROUPS:
-                load(i + 2)
-            if i < N_GROUPS:
-                truncated_squares(i)
-            if i >= 1:
-                add_up_and_store(i - 1)
-            if i < N_GROUPS:
-                gate_and_quantise(i)
-            if i + 1 < N_GROUPS:
-                mask_and_transpose_x(i + 1)
-                transpose_g_and_z(i + 1)
-            if i < N_GROUPS:
-                combine_squares(i)
+        for i in range(N_GROUPS + 2):
+            for step in range(8):
+                if 1 <= i <= N_GROUPS:
+                    multiply(i - 1, step)
+                if step == 0 and i + 2 < N_GROUPS:
+                    load(i + 2)
+                if step < 4:
+                    if i >= 2:
+                        add_up(i - 2, step)
+                    if i < N_GROUPS:
+                        truncated_squares(i, step)
+                if step < 2 and i < N_GROUPS:
+                    gate(i, step)
+                if step == 2 and i < N_GROUPS:
+                    quantise(i)
+                if i + 1 < N_GROUPS:
+                    if step == 3:
+                        mask_x(i + 1)
+                    if step == 4:
+                        transpose_g(i + 1)
+                    if step == 5 or step == 6:
+                        transpose_z(i + 1, step - 5)
+                    if step == 7:
+                        transpose_x(i + 1)
+                if step >= 4 and i < N_GROUPS:
+                    combine_squares(i, step - 4)

@@ -84,8 +84,8 @@ def tile_bsplinekanlayer_t_v_kernel(tc, x, coeff, base_weight, knots, z, grad_ou
         terms = stack.enter_context(tc.tile_pool(name="terms", bufs=2))
         results = stack.enter_context(tc.tile_pool(name="results", bufs=2))
         psum_x = stack.enter_context(tc.psum_pool(name="psum_x", bufs=1))
-        psum_in = stack.enter_context(tc.psum_pool(name="psum_in", bufs=2))
-        psum_mx = stack.enter_context(tc.psum_pool(name="psum_mx", bufs=4))
+        psum_in = stack.enter_context(tc.psum_pool(name="psum_in", bufs=3))
+        psum_mx = stack.enter_context(tc.psum_pool(name="psum_mx", bufs=3))
         psum_out = stack.enter_context(tc.psum_pool(name="psum_out", bufs=1))
         stack.enter_context(tc.manual_schedule())
 
@@ -192,17 +192,16 @@ def tile_bsplinekanlayer_t_v_kernel(tc, x, coeff, base_weight, knots, z, grad_ou
             if factor == 1:
                 twice_dz = grouped.tile([P, GROUP * PACK], BF16, align_bytes=64)
                 doubled[j] = twice_dz
-            for cols in (slice(0, HALF * PACK), slice(HALF * PACK, GROUP * PACK)):
-                if factor == 0:
-                    nc.vector.scalar_tensor_tensor(
-                        out=tanh_part[:, cols], in0=tanh_part[:, cols], scalar=1.0,
-                        in1=g_grouped[:, cols], op0=ALU.subtract, op1=ALU.mult,
-                    )
-                else:
-                    nc.vector.scalar_tensor_tensor(
-                        out=doubled[j][:, cols], in0=silu_part[:, cols], scalar=1.0,
-                        in1=tanh_part[:, cols], op0=ALU.subtract, op1=ALU.mult,
-                    )
+            if factor == 0:
+                nc.vector.scalar_tensor_tensor(
+                    out=tanh_part[:], in0=tanh_part[:], scalar=1.0, in1=g_grouped[:],
+                    op0=ALU.subtract, op1=ALU.mult,
+                )
+            else:
+                nc.vector.scalar_tensor_tensor(
+                    out=doubled[j][:], in0=silu_part[:], scalar=1.0, in1=tanh_part[:],
+                    op0=ALU.subtract, op1=ALU.mult,
+                )
 
         def quantise(j):
             g_codes = quantised.tile([P, GROUP], U32, align_bytes=64)

@@ -117,7 +117,7 @@ def tile_bsplinekanlayer_t_v_kernel(tc, x, coeff, base_weight, knots, z, grad_ou
         def mask_x(j):
             x_sb = loaded[j][0]
             push = masked.tile([P, 2, GROUP], BF16)
-            x_masked = masked.tile([P, 2, GROUP], BF16)
+            x_masked = masked.tile([P, GROUP], BF16)
             nc.vector.tensor_scalar(
                 out=push[:, 0, :], in0=x_sb[:], scalar1=t[:, HI : HI + 1], scalar2=-HUGE,
                 op0=ALU.is_ge, op1=ALU.mult,
@@ -126,26 +126,34 @@ def tile_bsplinekanlayer_t_v_kernel(tc, x, coeff, base_weight, knots, z, grad_ou
                 out=push[:, 1, :], in0=x_sb[:], scalar1=t[:, LO : LO + 1], scalar2=HUGE,
                 op0=ALU.is_le, op1=ALU.mult,
             )
-            for copy in range(2):
-                nc.vector.tensor_tensor(
-                    out=x_masked[:, copy, :], in0=x_sb[:], in1=push[:, copy, :], op=ALU.add
-                )
-            x_pushed[j] = x_masked
+            nc.vector.tensor_tensor(out=x_masked[:], in0=x_sb[:], in1=push[:, 1, :], op=ALU.add)
+            x_pushed[j] = (push, x_masked)
 
         def transpose_x(j):
             x_t = psum_x.tile([P, 2, GROUP], BF16)
-            for copy in range(2):
-                for tt in range(TILES):
-                    cols = slice(tt * P, (tt + 1) * P)
-                    nc.tensor.transpose(
-                        out=x_t[:, copy, cols], in_=x_pushed[j][:, copy, cols], identity=ident_bf[:]
-                    )
+            push, x_masked = x_pushed[j]
+            for tt in range(TILES):
+                cols = slice(tt * P, (tt + 1) * P)
+                nc.tensor.matmul(
+                    out=x_t[:, 0, cols], lhsT=loaded[j][0][:, cols], rhs=ident_bf[:],
+                    start=True, stop=False,
+                )
+                nc.tensor.matmul(
+                    out=x_t[:, 0, cols], lhsT=push[:, 0, cols], rhs=ident_bf[:],
+                    start=False, stop=True,
+                )
+            for tt in range(TILES):
+                cols = slice(tt * P, (tt + 1) * P)
+                nc.tensor.transpose(
+                    out=x_t[:, 1, cols], in_=x_masked[:, cols], identity=ident_bf[:]
+                )
             x_transposed[j] = x_t
 
         def transpose_g(j):
             g_words = loaded[j][1][:].bitcast(F32)
-            g_grouped = grouped.tile([P, GROUP * PACK], BF16, align_bytes=64)
-            g_grouped_words = g_grouped[:].bitcast(F32).rearrange("p (n u) -> p n u", u=2)
+            both = grouped.tile([P, 2 * GROUP * PACK], BF16, align_bytes=64)
+            g_grouped = both[:, 0 : GROUP * PACK]
+            g_grouped_words = g_grouped.bitcast(F32).rearrange("p (n u) -> p n u", u=2)
             for half in range(2):
                 g_t = psum_in.tile([P, 2, 2, P], F32, tag="in")
                 for tt in range(2):
@@ -164,6 +172,7 @@ def tile_bsplinekanlayer_t_v_kernel(tc, x, coeff, base_weight, knots, z, grad_ou
             tanh_part = gates.tile([P, GROUP * PACK], F32)
             silu_part = gates.tile([P, GROUP * PACK], F32)
             gate_parts[j] = (g_grouped, tanh_part, silu_part)
+            doubled[j] = both
 
         def transpose_z(j, half):
             z_view = loaded[j][2][:].rearrange("p (t u q e) -> p t u e q", t=TILES, u=2, e=2)
@@ -189,59 +198,57 @@ def tile_bsplinekanlayer_t_v_kernel(tc, x, coeff, base_weight, knots, z, grad_ou
 
         def gate(j, factor):
             g_grouped, tanh_part, silu_part = gate_parts[j]
-            if factor == 1:
-                twice_dz = grouped.tile([P, GROUP * PACK], BF16, align_bytes=64)
-                doubled[j] = twice_dz
             if factor == 0:
                 nc.vector.scalar_tensor_tensor(
-                    out=tanh_part[:], in0=tanh_part[:], scalar=1.0, in1=g_grouped[:],
+                    out=tanh_part[:], in0=tanh_part[:], scalar=1.0, in1=g_grouped,
                     op0=ALU.subtract, op1=ALU.mult,
                 )
             else:
                 nc.vector.scalar_tensor_tensor(
-                    out=doubled[j][:], in0=silu_part[:], scalar=1.0, in1=tanh_part[:],
+                    out=doubled[j][:, GROUP * PACK :], in0=silu_part[:], scalar=1.0,
+                    in1=tanh_part[:],
                     op0=ALU.subtract, op1=ALU.mult,
                 )
 
         def quantise(j):
-            g_codes = quantised.tile([P, GROUP], U32, align_bytes=64)
-            g_scales = quantised.tile([P, GROUP], U8, align_bytes=64)
+            codes = quantised.tile([P, 2 * GROUP], U32, align_bytes=64)
+            scales = quantised.tile([P, 2 * GROUP], U8, align_bytes=64)
             nc.vector.quantize_mx(
-                out=g_codes[:].bitcast(E5M2_X4), scales=g_scales[:], in_=gate_parts[j][0][:]
+                out=codes[:].bitcast(E5M2_X4), scales=scales[:], in_=doubled[j][:]
             )
-            dz_codes = quantised.tile([P, GROUP], U32, align_bytes=64)
-            dz_scales = quantised.tile([P, GROUP], U8, align_bytes=64)
-            nc.vector.quantize_mx(
-                out=dz_codes[:].bitcast(E5M2_X4), scales=dz_scales[:], in_=doubled[j][:]
+            operands[j] = (
+                codes[:, 0:GROUP], scales[:, 0:GROUP], codes[:, GROUP:], scales[:, GROUP:]
             )
-            operands[j] = (g_codes, g_scales, dz_codes, dz_scales)
 
         def truncated_squares(j, quarter):
             if quarter == 0:
-                rise = {}
-                fall = {}
-                for k in range(LO + 1, HI):
-                    rise[k] = squares.tile([P, GROUP], F32, name="rise%d" % k)
-                for k in range(LO + 1, HI - 1):
-                    fall[k] = squares.tile([P, GROUP], F32, name="fall%d" % k)
-                shapes[j] = (rise, fall)
-            rise, fall = shapes[j]
+                rises = squares.tile([P, HI - LO - 1, GROUP], F32)
+                falls = squares.tile([P, HI - LO - 2, GROUP], F32)
+                rise = dict([(k, rises[:, k - LO - 1, :]) for k in range(LO + 1, HI)])
+                fall = dict([(k, falls[:, k - LO - 1, :]) for k in range(LO + 1, HI - 1)])
+                shapes[j] = (rise, fall, rises, falls)
+            rise, fall, rises, falls = shapes[j]
             x_t = x_transposed[j]
-            ramps = [(rise[k], x_t[:, 0, :], 1.0, neg_t[:, k : k + 1]) for k in range(LO + 1, HI)]
-            ramps += [(fall[k], x_t[:, 1, :], -1.0, t[:, k : k + 1]) for k in range(LO + 1, HI - 1)]
-            for n in share(2 * len(ramps), quarter, 4):
-                if n < len(ramps):
-                    square, source, sign, shift = ramps[n]
+            if quarter == 0:
+                for k in range(LO + 1, HI):
                     nc.scalar.activation(
-                        out=square[:], in_=source, func=ACT.Relu, scale=sign, bias=shift
+                        out=rise[k], in_=x_t[:, 0, :], func=ACT.Relu, scale=1.0,
+                        bias=neg_t[:, k : k + 1],
                     )
-                else:
-                    square = ramps[n - len(ramps)][0]
-                    nc.scalar.activation(out=square[:], in_=square[:], func=ACT.Square)
+            if quarter == 1:
+                nc.scalar.activation(out=rises[:], in_=rises[:], func=ACT.Square)
+            if quarter == 2:
+                for k in range(LO + 1, HI - 1):
+                    nc.scalar.activation(
+                        out=fall[k], in_=x_t[:, 1, :], func=ACT.Relu, scale=-1.0,
+                        bias=t[:, k : k + 1],
+                    )
+            if quarter == 3:
+                nc.scalar.activation(out=falls[:], in_=falls[:], func=ACT.Square)
 
         def combine_squares(j, quarter):
-            rise, fall = shapes[j]
-            rise_steps = [(rise[r], rise[k], k - r, r) for r in range(4, 7) for k in range(r + 1, HI)]
+            rise, fall = shapes[j][0:2]
+            rise_steps = [(rise[r], rise[k], k - r, r) for k in range(5, HI) for r in range(4, k)]
             fall_steps = [
                 (fall[r + 4], fall[k], k - r, r) for r in (2, 1) for k in range(LO + 1, r + 4)
             ]
@@ -252,7 +259,7 @@ def tile_bsplinekanlayer_t_v_kernel(tc, x, coeff, base_weight, knots, z, grad_ou
             for n in share(len(steps), quarter, 4):
                 target, square, jj, r = steps[n]
                 nc.vector.scalar_tensor_tensor(
-                    out=target[:], in0=square[:], scalar=ratio[:, jj, r : r + 1], in1=target[:],
+                    out=target, in0=square, scalar=ratio[:, jj, r : r + 1], in1=target,
                     op0=ALU.mult, op1=ALU.add,
                 )
 
@@ -262,14 +269,14 @@ def tile_bsplinekanlayer_t_v_kernel(tc, x, coeff, base_weight, knots, z, grad_ou
 
         def multiply(j, n_term):
             g_codes, g_scales, dz_codes, dz_scales = operands[j]
-            rise, fall = shapes[j]
+            rise, fall = shapes[j][0:2]
             bank = psum_mx.tile([P, GROUP], F32, tag="mx")
             term = terms.tile([P, GROUP], F32, name="term%d" % n_term)
             if n_term == 0:
                 codes, scales = part(BASE)
                 nc.tensor.matmul_mx(
                     out=bank[:], lhsT=codes, lhsT_scale=scales,
-                    rhs=dz_codes[:].bitcast(E5M2_X4), rhs_scale=dz_scales[:], start=True, stop=True,
+                    rhs=dz_codes.bitcast(E5M2_X4), rhs_scale=dz_scales, start=True, stop=True,
                 )
                 nc.scalar.activation(out=term[:], in_=bank[:], func=ACT.Copy, scale=0.5)
                 summands[j] = [term]
@@ -279,12 +286,12 @@ def tile_bsplinekanlayer_t_v_kernel(tc, x, coeff, base_weight, knots, z, grad_ou
                     codes, scales = part(n)
                     nc.tensor.matmul_mx(
                         out=bank[:], lhsT=codes, lhsT_scale=scales,
-                        rhs=g_codes[:].bitcast(E5M2_X4), rhs_scale=g_scales[:],
+                        rhs=g_codes.bitcast(E5M2_X4), rhs_scale=g_scales,
                         start=(n == r), stop=(n == NEGATED),
                     )
                 shape = rise[r] if r >= 4 else fall[r + 4]
                 nc.vector.scalar_tensor_tensor(
-                    out=term[:], in0=bank[:], scalar=lead[:, r : r + 1], in1=shape[:],
+                    out=term[:], in0=bank[:], scalar=lead[:, r : r + 1], in1=shape,
                     op0=ALU.mult, op1=ALU.mult,
                 )
                 summands[j].append(term)

@@ -45,12 +45,19 @@ def spline_weights(nc, consts, t):
         gap.append(gap_d)
 
     size = consts.tile([P, 5, N_BASIS], F32)
+    factors = []
     for j in range(5):
-        factors = [gap[j - l - 1][:, l : l + N_BASIS] for l in range(j)]
-        factors += [gap[l - j - 1][:, j : j + N_BASIS] for l in range(j + 1, 5)]
-        nc.vector.tensor_tensor(out=size[:, j, :], in0=factors[0], in1=factors[1], op=ALU.mult)
-        for factor in factors[2:]:
-            nc.vector.tensor_tensor(out=size[:, j, :], in0=size[:, j, :], in1=factor, op=ALU.mult)
+        factors.append([gap[j - l - 1][:, l : l + N_BASIS] for l in range(j)])
+        factors[j] += [gap[l - j - 1][:, j : j + N_BASIS] for l in range(j + 1, 5)]
+    for j in range(5):
+        nc.vector.tensor_tensor(
+            out=size[:, j, :], in0=factors[j][0], in1=factors[j][1], op=ALU.mult
+        )
+    for n in (2, 3):
+        for j in range(5):
+            nc.vector.tensor_tensor(
+                out=size[:, j, :], in0=size[:, j, :], in1=factors[j][n], op=ALU.mult
+            )
     inverse = consts.tile([P, 5, N_BASIS], F32)
     nc.vector.reciprocal(out=inverse[:], in_=size[:])
 
@@ -119,12 +126,12 @@ def tile_bsplinekanlayer_t_v_kernel(tc, x, coeff, base_weight, knots, z, grad_ou
             push = masked.tile([P, 2, GROUP], BF16)
             x_masked = masked.tile([P, GROUP], BF16)
             nc.vector.tensor_scalar(
-                out=push[:, 0, :], in0=x_sb[:], scalar1=t[:, HI : HI + 1], scalar2=-HUGE,
-                op0=ALU.is_ge, op1=ALU.mult,
-            )
-            nc.vector.tensor_scalar(
                 out=push[:, 1, :], in0=x_sb[:], scalar1=t[:, LO : LO + 1], scalar2=HUGE,
                 op0=ALU.is_le, op1=ALU.mult,
+            )
+            nc.vector.tensor_scalar(
+                out=push[:, 0, :], in0=x_sb[:], scalar1=t[:, HI : HI + 1], scalar2=-HUGE,
+                op0=ALU.is_ge, op1=ALU.mult,
             )
             nc.vector.tensor_tensor(out=x_masked[:], in0=x_sb[:], in1=push[:, 1, :], op=ALU.add)
             x_pushed[j] = (push, x_masked)
@@ -235,9 +242,9 @@ def tile_bsplinekanlayer_t_v_kernel(tc, x, coeff, base_weight, knots, z, grad_ou
                         out=rise[k], in_=x_t[:, 0, :], func=ACT.Relu, scale=1.0,
                         bias=neg_t[:, k : k + 1],
                     )
-            if quarter == 1:
-                nc.scalar.activation(out=rises[:], in_=rises[:], func=ACT.Square)
             if quarter == 2:
+                nc.scalar.activation(out=rises[:], in_=rises[:], func=ACT.Square)
+            if quarter == 1:
                 for k in range(LO + 1, HI - 1):
                     nc.scalar.activation(
                         out=fall[k], in_=x_t[:, 1, :], func=ACT.Relu, scale=-1.0,
@@ -314,6 +321,31 @@ def tile_bsplinekanlayer_t_v_kernel(tc, x, coeff, base_weight, knots, z, grad_ou
                     out=out[rows, :].rearrange("(p t) i -> p t i", t=TILES), in_=out_sb[:]
                 )
 
+        def add_up_last(j, n):
+            if n == 0:
+                sum0 = psum_in.tile([P, P], F32, tag="in")
+                sum1 = psum_in.tile([P, P], F32, tag="in")
+                sum2 = psum_in.tile([P, P], F32, tag="in")
+                x_t = psum_x.tile([P, P], F32)
+                totals[j] = (sum0, sum1, sum2, x_t)
+            last = len(KEPT)
+            for tt in range(TILES):
+                nc.tensor.matmul(
+                    out=totals[j][tt][:], lhsT=summands[j][n][:, tt * P : (tt + 1) * P],
+                    rhs=ident_f32[:], is_transpose=True, start=(n == 0), stop=(n == last),
+                )
+            if n == last:
+                out_sb = results.tile([P, TILES, P], F32)
+                for tt in range(TILES):
+                    if tt % 2 == 0:
+                        nc.scalar.copy(out=out_sb[:, tt, :], in_=totals[j][tt][:])
+                    else:
+                        nc.vector.tensor_copy(out=out_sb[:, tt, :], in_=totals[j][tt][:])
+                rows = slice(j * GROUP, (j + 1) * GROUP)
+                nc.sync.dma_start(
+                    out=out[rows, :].rearrange("(p t) i -> p t i", t=TILES), in_=out_sb[:]
+                )
+
         knots_bf = consts.tile([P, N_KNOTS], BF16)
         nc.sync.dma_start(out=knots_bf[:], in_=knots.partition_broadcast(P))
         load(0)
@@ -379,10 +411,12 @@ def tile_bsplinekanlayer_t_v_kernel(tc, x, coeff, base_weight, knots, z, grad_ou
                 in_=weight_grouped[:, pair * 2 * P * PACK : (pair + 1) * 2 * P * PACK],
             )
 
-        for i in range(N_GROUPS + 2):
+        for i in range(N_GROUPS + 1):
             for step in range(8):
-                if 1 <= i <= N_GROUPS:
+                if i >= 1:
                     multiply(i - 1, step)
+                if i == N_GROUPS and step >= 1:
+                    add_up_last(i - 1, step - 1)
                 if step == 0 and i + 2 < N_GROUPS:
                     load(i + 2)
                 if step < 4:
@@ -405,3 +439,4 @@ def tile_bsplinekanlayer_t_v_kernel(tc, x, coeff, base_weight, knots, z, grad_ou
                         transpose_x(i + 1)
                 if step >= 4 and i < N_GROUPS:
                     combine_squares(i, step - 4)
+        add_up_last(N_GROUPS - 1, len(KEPT))

@@ -388,7 +388,8 @@ def tile_bsplinekanlayer_t_v_kernel(tc, x, coeff, base_weight, knots, z, grad_ou
         weight_grouped_words = weight_grouped[:].bitcast(F32).rearrange("p (n u) -> p n u", u=2)
         weight_codes = consts.tile([P, N_PARTS * P], U32, align_bytes=64)
         weight_scales = consts.tile([P, N_PARTS * P], U8, align_bytes=64)
-        for pair in range(N_PARTS // 2):
+
+        def transpose_weights(pair):
             weight_t = psum_in.tile([P, 2, 2, P], F32, tag="in")
             for nn in range(2):
                 for u in range(2):
@@ -403,13 +404,20 @@ def tile_bsplinekanlayer_t_v_kernel(tc, x, coeff, base_weight, knots, z, grad_ou
                 ),
                 in_=weight_t[:].rearrange("p n u i -> p n i u"),
             )
-        for pair in range(N_PARTS // 2):
-            cols = slice(pair * 2 * P, (pair + 1) * 2 * P)
+
+        for pair in (0, 1, 4):
+            transpose_weights(pair)
+        gate(0, 0)
+        for pair in (2, 3):
+            transpose_weights(pair)
+        gate(0, 1)
+        for first, end in ((0, 8), (8, N_PARTS)):
             nc.vector.quantize_mx(
-                out=weight_codes[:, cols].bitcast(E4M3_X4),
-                scales=weight_scales[:, cols],
-                in_=weight_grouped[:, pair * 2 * P * PACK : (pair + 1) * 2 * P * PACK],
+                out=weight_codes[:, first * P : end * P].bitcast(E4M3_X4),
+                scales=weight_scales[:, first * P : end * P],
+                in_=weight_grouped[:, first * P * PACK : end * P * PACK],
             )
+        quantise(0)
 
         for i in range(N_GROUPS + 1):
             for step in range(8):
@@ -424,9 +432,9 @@ def tile_bsplinekanlayer_t_v_kernel(tc, x, coeff, base_weight, knots, z, grad_ou
                         add_up(i - 2, step)
                     if i < N_GROUPS:
                         truncated_squares(i, step)
-                if step < 2 and i < N_GROUPS:
+                if step < 2 and 1 <= i < N_GROUPS:
                     gate(i, step)
-                if step == 2 and i < N_GROUPS:
+                if step == 2 and 1 <= i < N_GROUPS:
                     quantise(i)
                 if i + 1 < N_GROUPS:
                     if step == 3:

@@ -94,7 +94,6 @@ def tile_bsplinekanlayer_t_v_kernel(tc, x, coeff, base_weight, knots, z, grad_ou
         psum_in = stack.enter_context(tc.psum_pool(name="psum_in", bufs=3))
         psum_mx = stack.enter_context(tc.psum_pool(name="psum_mx", bufs=3))
         psum_out = stack.enter_context(tc.psum_pool(name="psum_out", bufs=1))
-        stack.enter_context(tc.manual_schedule())
 
         loaded = {}
         x_transposed = {}

from contextlib import ExitStack

import concourse.mybir as mybir
from concourse.masks import make_identity

F32 = mybir.dt.float32
BF16 = mybir.dt.bfloat16
U32 = mybir.dt.uint32
U8 = mybir.dt.uint8
E4M3_X4 = mybir.dt.float8_e4m3fn_x4
E5M2_X4 = mybir.dt.float8_e5m2_x4
ALU = mybir.AluOpType
ACT = mybir.ActivationFunctionType

P = 128
TOKENS = 8192
N_OUT = 512
N_BASIS = 8
N_KNOTS = 12
LO = 3
HI = 8
PACK = 4
GROUP = 512
TILES = GROUP // P
N_GROUPS = TOKENS // GROUP
HALF = GROUP // 2
HUGE = 3.0e38

DROPPED = 3
KEPT = (0, 1, 2, 4, 5, 6, 7)
NEGATED = 8
BASE = 9
N_PARTS = 10

FLOPS = 2 * TOKENS * N_OUT * (P * N_BASIS + P)


def spline_weights(nc, consts, t):
    gap = []
    for d in range(1, 5):
        gap_d = consts.tile([P, N_KNOTS - d], F32, name="gap%d" % d)
        nc.vector.tensor_tensor(
            out=gap_d[:], in0=t[:, d:N_KNOTS], in1=t[:, 0 : N_KNOTS - d], op=ALU.subtract
        )
        gap.append(gap_d)

    size = consts.tile([P, 5, N_BASIS], F32)
    factors = []
    for j in range(5):
        factors.append([gap[j - l - 1][:, l : l + N_BASIS] for l in range(j)])
        factors[j] += [gap[l - j - 1][:, j : j + N_BASIS] for l in range(j + 1, 5)]
    for j in range(5):
        nc.vector.tensor_tensor(
            out=size[:, j, :], in0=factors[j][0], in1=factors[j][1], op=ALU.mult
        )
    for n in (2, 3):
        for j in range(5):
            nc.vector.tensor_tensor(
                out=size[:, j, :], in0=size[:, j, :], in1=factors[j][n], op=ALU.mult
            )
    inverse = consts.tile([P, 5, N_BASIS], F32)
    nc.vector.reciprocal(out=inverse[:], in_=size[:])

    span = gap[3]
    lead = consts.tile([P, N_BASIS], F32)
    ratio = consts.tile([P, 5, N_BASIS], F32)
    for splines, leading, degree in ((slice(0, 4), 4, -3.0), (slice(4, 8), 0, 3.0)):
        nc.vector.scalar_tensor_tensor(
            out=lead[:, splines], in0=inverse[:, leading, splines], scalar=degree,
            in1=span[:, splines], op0=ALU.mult, op1=ALU.mult,
        )
        for j in range(1, 4):
            nc.vector.scalar_tensor_tensor(
                out=ratio[:, j, splines], in0=inverse[:, j, splines],
                scalar=(-1.0 if j % 2 else 1.0), in1=size[:, leading, splines],
                op0=ALU.mult, op1=ALU.mult,
            )
    return lead, ratio


def tile_bsplinekanlayer_t_v_kernel(tc, x, coeff, base_weight, knots, z, grad_out, out):
    nc = tc.nc
    with ExitStack() as stack:
        consts = stack.enter_context(tc.tile_pool(name="consts", bufs=1))
        loads = stack.enter_context(tc.tile_pool(name="loads", bufs=3))
        masked = stack.enter_context(tc.tile_pool(name="masked", bufs=2))
        gates = stack.enter_context(tc.tile_pool(name="gates", bufs=2))
        grouped = stack.enter_context(tc.tile_pool(name="grouped", bufs=2))
        quantised = stack.enter_context(tc.tile_pool(name="quantised", bufs=2))
        squares = stack.enter_context(tc.tile_pool(name="squares", bufs=2))
        terms = stack.enter_context(tc.tile_pool(name="terms", bufs=2))
        results = stack.enter_context(tc.tile_pool(name="results", bufs=2))
        psum_x = stack.enter_context(tc.psum_pool(name="psum_x", bufs=1))
        psum_in = stack.enter_context(tc.psum_pool(name="psum_in", bufs=3))
        psum_mx = stack.enter_context(tc.psum_pool(name="psum_mx", bufs=3))
        psum_out = stack.enter_context(tc.psum_pool(name="psum_out", bufs=1))

        loaded = {}
        x_transposed = {}
        gate_parts = {}
        operands = {}
        shapes = {}
        summands = {}
        x_pushed = {}
        doubled = {}
        totals = {}

        def load(j):
            rows = slice(j * GROUP, (j + 1) * GROUP)
            x_sb = loads.tile([P, GROUP], BF16)
            nc.sync.dma_start(out=x_sb[:], in_=x[rows, :].rearrange("(p t) i -> p (t i)", t=TILES))
            g_sb = loads.tile([P, TILES * N_OUT], BF16)
            nc.sync.dma_start(
                out=g_sb[:], in_=grad_out[rows, :].rearrange("(p t) o -> p (t o)", t=TILES)
            )
            z_sb = loads.tile([P, TILES * N_OUT], F32)
            nc.sync.dma_start(out=z_sb[:], in_=z[rows, :].rearrange("(p t) o -> p (t o)", t=TILES))
            loaded[j] = (x_sb, g_sb, z_sb)

        def share(count, piece, pieces):
            return range(count * piece // pieces, count * (piece + 1) // pieces)

        def mask_x(j):
            x_sb = loaded[j][0]
            push = masked.tile([P, 2, GROUP], BF16)
            x_masked = masked.tile([P, GROUP], BF16)
            nc.vector.tensor_scalar(
                out=push[:, 1, :], in0=x_sb[:], scalar1=t[:, LO : LO + 1], scalar2=HUGE,
                op0=ALU.is_le, op1=ALU.mult,
            )
            nc.vector.tensor_scalar(
                out=push[:, 0, :], in0=x_sb[:], scalar1=t[:, HI : HI + 1], scalar2=-HUGE,
                op0=ALU.is_ge, op1=ALU.mult,
            )
            nc.vector.tensor_tensor(out=x_masked[:], in0=x_sb[:], in1=push[:, 1, :], op=ALU.add)
            x_pushed[j] = (push, x_masked)

        def transpose_x(j):
            x_t = psum_x.tile([P, 2, GROUP], BF16)
            push, x_masked = x_pushed[j]
            for tt in range(TILES):
                cols = slice(tt * P, (tt + 1) * P)
                nc.tensor.matmul(
                    out=x_t[:, 0, cols], lhsT=loaded[j][0][:, cols], rhs=ident_bf[:],
                    start=True, stop=False,
                )
                nc.tensor.matmul(
                    out=x_t[:, 0, cols], lhsT=push[:, 0, cols], rhs=ident_bf[:],
                    start=False, stop=True,
                )
            for tt in range(TILES):
                cols = slice(tt * P, (tt + 1) * P)
                nc.tensor.transpose(
                    out=x_t[:, 1, cols], in_=x_masked[:, cols], identity=ident_bf[:]
                )
            x_transposed[j] = x_t

        def transpose_g(j):
            g_words = loaded[j][1][:].bitcast(F32)
            both = grouped.tile([P, 2 * GROUP * PACK], BF16, align_bytes=64)
            g_grouped = both[:, 0 : GROUP * PACK]
            g_grouped_words = g_grouped.bitcast(F32).rearrange("p (n u) -> p n u", u=2)
            for half in range(2):
                g_t = psum_in.tile([P, 2, 2, P], F32, tag="in")
                for tt in range(2):
                    for u in range(2):
                        first = (2 * half + tt) * (N_OUT // 2) + u * P
                        nc.tensor.transpose(
                            out=g_t[:, tt, u, :], in_=g_words[:, first : first + P],
                            identity=ident_f32[:],
                        )
                nc.scalar.copy(
                    out=g_grouped_words[:, half * HALF : (half + 1) * HALF, :].rearrange(
                        "p (t k) u -> p t k u", t=2
                    ),
                    in_=g_t[:].rearrange("p t u k -> p t k u"),
                )
            tanh_part = gates.tile([P, GROUP * PACK], F32)
            silu_part = gates.tile([P, GROUP * PACK], F32)
            gate_parts[j] = (g_grouped, tanh_part, silu_part)
            doubled[j] = both

        def transpose_z(j, half):
            z_view = loaded[j][2][:].rearrange("p (t u q e) -> p t u e q", t=TILES, u=2, e=2)
            tanh_part = gate_parts[j][1]
            silu_part = gate_parts[j][2]
            for tt in (2 * half, 2 * half + 1):
                z_t = psum_in.tile([P, PACK, P], F32, tag="in")
                for u in range(2):
                    for e in range(2):
                        nc.tensor.transpose(
                            out=z_t[:, 2 * u + e, :], in_=z_view[:, tt, u, e, :],
                            identity=ident_f32[:],
                        )
                cols = slice(tt * P * PACK, (tt + 1) * P * PACK)
                nc.scalar.activation(
                    out=tanh_part[:, cols].rearrange("p (k c) -> p k c", c=PACK),
                    in_=z_t[:].rearrange("p c k -> p k c"), func=ACT.Tanh, scale=-0.5,
                )
                nc.scalar.activation(
                    out=silu_part[:, cols].rearrange("p (k c) -> p k c", c=PACK),
                    in_=z_t[:].rearrange("p c k -> p k c"), func=ACT.Silu, scale=-1.0,
                )

        def gate(j, factor):
            g_grouped, tanh_part, silu_part = gate_parts[j]
            if factor == 0:
                nc.vector.scalar_tensor_tensor(
                    out=tanh_part[:], in0=tanh_part[:], scalar=1.0, in1=g_grouped,
                    op0=ALU.subtract, op1=ALU.mult,
                )
            else:
                nc.vector.scalar_tensor_tensor(
                    out=doubled[j][:, GROUP * PACK :], in0=silu_part[:], scalar=1.0,
                    in1=tanh_part[:],
                    op0=ALU.subtract, op1=ALU.mult,
                )

        def quantise(j):
            codes = quantised.tile([P, 2 * GROUP], U32, align_bytes=64)
            scales = quantised.tile([P, 2 * GROUP], U8, align_bytes=64)
            nc.vector.quantize_mx(
                out=codes[:].bitcast(E5M2_X4), scales=scales[:], in_=doubled[j][:]
            )
            operands[j] = (
                codes[:, 0:GROUP], scales[:, 0:GROUP], codes[:, GROUP:], scales[:, GROUP:]
            )

        def truncated_squares(j, quarter):
            if quarter == 0:
                rises = squares.tile([P, HI - LO - 1, GROUP], F32)
                falls = squares.tile([P, HI - LO - 2, GROUP], F32)
                rise = dict([(k, rises[:, k - LO - 1, :]) for k in range(LO + 1, HI)])
                fall = dict([(k, falls[:, k - LO - 1, :]) for k in range(LO + 1, HI - 1)])
                shapes[j] = (rise, fall, rises, falls)
            rise, fall, rises, falls = shapes[j]
            x_t = x_transposed[j]
            if quarter == 0:
                for k in range(LO + 1, HI):
                    nc.scalar.activation(
                        out=rise[k], in_=x_t[:, 0, :], func=ACT.Relu, scale=1.0,
                        bias=neg_t[:, k : k + 1],
                    )
            if quarter == 2:
                nc.scalar.activation(out=rises[:], in_=rises[:], func=ACT.Square)
            if quarter == 1:
                for k in range(LO + 1, HI - 1):
                    nc.scalar.activation(
                        out=fall[k], in_=x_t[:, 1, :], func=ACT.Relu, scale=-1.0,
                        bias=t[:, k : k + 1],
                    )
            if quarter == 3:
                nc.scalar.activation(out=falls[:], in_=falls[:], func=ACT.Square)

        def combine_squares(j, quarter):
            rise, fall = shapes[j][0:2]
            rise_steps = [(rise[r], rise[k], k - r, r) for k in range(5, HI) for r in range(4, k)]
            fall_steps = [
                (fall[r + 4], fall[k], k - r, r) for r in (2, 1) for k in range(LO + 1, r + 4)
            ]
            steps = []
            for n, step in enumerate(rise_steps):
                steps.append(step)
                steps.extend(fall_steps[n : n + 1])
            for n in share(len(steps), quarter, 4):
                target, square, jj, r = steps[n]
                nc.vector.scalar_tensor_tensor(
                    out=target, in0=square, scalar=ratio[:, jj, r : r + 1], in1=target,
                    op0=ALU.mult, op1=ALU.add,
                )

        def part(n):
            cols = slice(n * P, (n + 1) * P)
            return weight_codes[:, cols].bitcast(E4M3_X4), weight_scales[:, cols]

        def multiply(j, n_term):
            g_codes, g_scales, dz_codes, dz_scales = operands[j]
            rise, fall = shapes[j][0:2]
            bank = psum_mx.tile([P, GROUP], F32, tag="mx")
            term = terms.tile([P, GROUP], F32, name="term%d" % n_term)
            if n_term == 0:
                codes, scales = part(BASE)
                nc.tensor.matmul_mx(
                    out=bank[:], lhsT=codes, lhsT_scale=scales,
                    rhs=dz_codes.bitcast(E5M2_X4), rhs_scale=dz_scales, start=True, stop=True,
                )
                nc.scalar.activation(out=term[:], in_=bank[:], func=ACT.Copy, scale=0.5)
                summands[j] = [term]
            else:
                r = KEPT[n_term - 1]
                for n in (r, NEGATED):
                    codes, scales = part(n)
                    nc.tensor.matmul_mx(
                        out=bank[:], lhsT=codes, lhsT_scale=scales,
                        rhs=g_codes.bitcast(E5M2_X4), rhs_scale=g_scales,
                        start=(n == r), stop=(n == NEGATED),
                    )
                shape = rise[r] if r >= 4 else fall[r + 4]
                nc.vector.scalar_tensor_tensor(
                    out=term[:], in0=bank[:], scalar=lead[:, r : r + 1], in1=shape,
                    op0=ALU.mult, op1=ALU.mult,
                )
                summands[j].append(term)

        def add_up(j, tt):
            if tt == 0:
                total = psum_out.tile([P, TILES, P], F32)
                totals[j] = total
            last = len(summands[j]) - 1
            for n, summand in enumerate(summands[j]):
                nc.tensor.matmul(
                    out=totals[j][:, tt, :], lhsT=summand[:, tt * P : (tt + 1) * P],
                    rhs=ident_f32[:], is_transpose=True, start=(n == 0), stop=(n == last),
                )
            if tt == TILES - 1:
                out_sb = results.tile([P, TILES, P], F32)
                nc.scalar.copy(out=out_sb[:], in_=totals[j][:])
                rows = slice(j * GROUP, (j + 1) * GROUP)
                nc.sync.dma_start(
                    out=out[rows, :].rearrange("(p t) i -> p t i", t=TILES), in_=out_sb[:]
                )

        def add_up_last(j, n):
            if n == 0:
                sum0 = psum_in.tile([P, P], F32, tag="in")
                sum1 = psum_in.tile([P, P], F32, tag="in")
                sum2 = psum_in.tile([P, P], F32, tag="in")
                x_t = psum_x.tile([P, P], F32)
                totals[j] = (sum0, sum1, sum2, x_t)
            last = len(KEPT)
            for tt in range(TILES):
                nc.tensor.matmul(
                    out=totals[j][tt][:], lhsT=summands[j][n][:, tt * P : (tt + 1) * P],
                    rhs=ident_f32[:], is_transpose=True, start=(n == 0), stop=(n == last),
                )
            if n == last:
                out_sb = results.tile([P, TILES, P], F32)
                for tt in range(TILES):
                    if tt % 2 == 0:
                        nc.scalar.copy(out=out_sb[:, tt, :], in_=totals[j][tt][:])
                    else:
                        nc.vector.tensor_copy(out=out_sb[:, tt, :], in_=totals[j][tt][:])
                rows = slice(j * GROUP, (j + 1) * GROUP)
                nc.sync.dma_start(
                    out=out[rows, :].rearrange("(p t) i -> p t i", t=TILES), in_=out_sb[:]
                )

        knots_bf = consts.tile([P, N_KNOTS], BF16)
        nc.sync.dma_start(out=knots_bf[:], in_=knots.partition_broadcast(P))
        load(0)
        coeff_sb = consts.tile([P, N_OUT, N_BASIS], BF16)
        nc.sync.dma_start(out=coeff_sb[:], in_=coeff)
        weight_sb = consts.tile([P, N_PARTS * N_OUT], BF16)
        weight_view = weight_sb[:].rearrange("p (n o) -> p n o", n=N_PARTS)
        nc.sync.dma_start(out=weight_view[:, BASE, :], in_=base_weight)
        load(1)

        ident_bf = consts.tile([P, P], BF16)
        make_identity(nc, ident_bf[:])
        ident_f32 = consts.tile([P, P], F32)
        make_identity(nc, ident_f32[:])

        transpose_g(0)
        transpose_z(0, 0)
        transpose_z(0, 1)

        t = consts.tile([P, N_KNOTS], F32)
        nc.vector.tensor_copy(out=t[:], in_=knots_bf[:])
        neg_t = consts.tile([P, N_KNOTS], F32)
        nc.vector.tensor_scalar(out=neg_t[:], in0=t[:], scalar1=-1.0, scalar2=None, op0=ALU.mult)
        mask_x(0)
        transpose_x(0)
        lead, ratio = spline_weights(nc, consts, t)

        nc.vector.tensor_copy(
            out=weight_view[:, 0:4, :], in_=coeff_sb[:, :, 0:4].rearrange("p o r -> p r o")
        )
        nc.scalar.copy(
            out=weight_view[:, 4:8, :], in_=coeff_sb[:, :, 4:8].rearrange("p o r -> p r o")
        )
        nc.vector.tensor_scalar(
            out=weight_view[:, NEGATED, :], in0=coeff_sb[:, :, DROPPED], scalar1=-1.0, scalar2=None,
            op0=ALU.mult,
        )
        weight_words = weight_sb[:].bitcast(F32)
        weight_grouped = consts.tile([P, N_PARTS * P * PACK], BF16, align_bytes=64)
        weight_grouped_words = weight_grouped[:].bitcast(F32).rearrange("p (n u) -> p n u", u=2)
        weight_codes = consts.tile([P, N_PARTS * P], U32, align_bytes=64)
        weight_scales = consts.tile([P, N_PARTS * P], U8, align_bytes=64)

        def transpose_weights(pair):
            weight_t = psum_in.tile([P, 2, 2, P], F32, tag="in")
            for nn in range(2):
                for u in range(2):
                    first = (2 * pair + nn) * (N_OUT // 2) + u * P
                    nc.tensor.transpose(
                        out=weight_t[:, nn, u, :], in_=weight_words[:, first : first + P],
                        identity=ident_f32[:],
                    )
            nc.vector.tensor_copy(
                out=weight_grouped_words[:, pair * 2 * P : (pair + 1) * 2 * P, :].rearrange(
                    "p (n i) u -> p n i u", n=2
                ),
                in_=weight_t[:].rearrange("p n u i -> p n i u"),
            )

        for pair in (0, 1, 4):
            transpose_weights(pair)
        gate(0, 0)
        for pair in (2, 3):
            transpose_weights(pair)
        gate(0, 1)
        for first, end in ((0, 8), (8, N_PARTS)):
            nc.vector.quantize_mx(
                out=weight_codes[:, first * P : end * P].bitcast(E4M3_X4),
                scales=weight_scales[:, first * P : end * P],
                in_=weight_grouped[:, first * P * PACK : end * P * PACK],
            )
        quantise(0)

        for i in range(N_GROUPS + 1):
            for step in range(8):
                if i >= 1:
                    multiply(i - 1, step)
                if i == N_GROUPS and step >= 1:
                    add_up_last(i - 1, step - 1)
                if step == 0 and i + 2 < N_GROUPS:
                    load(i + 2)
                if step < 4:
                    if i >= 2:
                        add_up(i - 2, step)
                    if i < N_GROUPS:
                        truncated_squares(i, step)
                if step < 2 and 1 <= i < N_GROUPS:
                    gate(i, step)
                if step == 2 and 1 <= i < N_GROUPS:
                    quantise(i)
                if i + 1 < N_GROUPS:
                    if step == 3:
                        mask_x(i + 1)
                    if step == 4:
                        transpose_g(i + 1)
                    if step == 5 or step == 6:
                        transpose_z(i + 1, step - 5)
                    if step == 7:
                        transpose_x(i + 1)
                if step >= 4 and i < N_GROUPS:
                    combine_squares(i, step - 4)
        add_up_last(N_GROUPS - 1, len(KEPT))
